import numpy as np
import ml_dtypes


def mxq(x, axis, fmt="e4m3"):
    dtype, down = {"e4m3": (ml_dtypes.float8_e4m3fn, 7), "e5m2": (ml_dtypes.float8_e5m2, 14)}[fmt]
    v = np.moveaxis(np.asarray(x, np.float32).astype(ml_dtypes.bfloat16).astype(np.float64), axis, -1)
    blocks = v.reshape(v.shape[:-1] + (-1, 32))
    amax = np.abs(blocks).max(-1, keepdims=True)
    byte = np.maximum(np.where(amax > 0, np.frexp(amax)[1] - 1 + 127, 0) - down, 1)
    scale = np.exp2(byte - 127.0)
    codes = (blocks / scale).astype(np.float32).astype(dtype).astype(np.float64)
    return np.moveaxis((codes * scale).reshape(v.shape), -1, axis)


WIDE = False


def mx_kscale(k):
    if not WIDE:
        return np.ones(k)
    levels = np.array([10, -10, 5, -5, 0])
    if k % 512:
        return np.exp2(np.random.permutation(np.resize(levels, k // 32))).repeat(32)
    a = np.empty((k // 512, 16))
    for p in range(k // 512):
        a[p, :8] = np.random.permutation(np.resize(levels, 8))
        for g in range(8):
            far = levels[np.abs(levels - a[p, g]) >= 10]
            a[p, g + 8] = far[np.random.randint(len(far))]
    return np.exp2(a.ravel()).repeat(32)


BF16 = ml_dtypes.bfloat16


def bf(x):
    return np.asarray(x, np.float32).astype(BF16)


def f64(x):
    return np.asarray(x).astype(np.float64)


B, H, A = 512, 1024, 1024


def setup_inputs():
    s = mx_kscale(H)
    return {
        "x": bf(np.random.standard_normal((B, H)) * s),
        "alpha": bf(np.random.standard_normal((B, H)) * s),
        "aa": bf(np.random.standard_normal((B, A)) * 0.5),
        "bb": bf(np.random.uniform(0.5, 1.5, (B, A))),
        "pp": bf(np.random.standard_normal((B, A))),
        "time_decay": bf(-1.0 + 1.5 * np.random.standard_normal(A)),
        "time_first": bf(-1.2 + 0.5 * np.random.standard_normal(A)),
        "time_mix_k": bf(np.random.uniform(0.1, 0.9, H)),
        "time_mix_v": bf(np.random.uniform(0.2, 1.1, H)),
        "Wk": bf(np.random.standard_normal((A, H)) * 1.5 / np.sqrt(H) / s),
        "Wv": bf(np.random.standard_normal((A, H)) * 1.2 / np.sqrt(H) / s),
    }


def reference(x, alpha, aa, bb, pp, time_decay, time_first, time_mix_k, time_mix_v, Wk, Wv):
    x, alpha, aa, bb, pp = f64(x), f64(alpha), f64(aa), f64(bb), f64(pp)
    time_decay, time_first = f64(time_decay), f64(time_first)
    time_mix_k, time_mix_v = f64(time_mix_k), f64(time_mix_v)
    xk = x * time_mix_k + alpha * (1.0 - time_mix_k)
    xv = x * time_mix_v + alpha * (1.0 - time_mix_v)
    k = mxq(xk, 1, "e4m3") @ mxq(f64(Wk), 1, "e4m3").T
    v = mxq(xv, 1, "e4m3") @ mxq(f64(Wv), 1, "e4m3").T
    ww = time_first + k
    qq = np.maximum(pp, ww)
    e1 = np.exp(pp - qq)
    e2 = np.exp(ww - qq)
    wkv = (e1 * aa + e2 * v) / (e1 * bb + e2)
    ww2 = pp + time_decay
    qq2 = np.maximum(ww2, k)
    e1b = np.exp(ww2 - qq2)
    e2b = np.exp(k - qq2)
    next_aa = e1b * aa + e2b * v
    next_bb = e1b * bb + e2b
    return (wkv, next_aa, next_bb, qq2)

@@ -1,0 +1,302 @@
+from contextlib import ExitStack
+
+import concourse.mybir as mybir
+from concourse.masks import make_identity
+
+F32 = mybir.dt.float32
+BF16 = mybir.dt.bfloat16
+U32 = mybir.dt.uint32
+U8 = mybir.dt.uint8
+FP8X4 = mybir.dt.float8_e4m3fn_x4
+ALU = mybir.AluOpType
+ACT = mybir.ActivationFunctionType
+
+B, H, A = 512, 1024, 1024
+P = 128
+ROW_TILES = B // P
+K_PASS = 4 * P
+PASSES = H // K_PASS
+N_TILE = 512
+COL_TILES = A // N_TILE
+PASS_WORDS = K_PASS // 2
+TINY = 2.0 ** -60
+
+FLOPS = 2 * 2 * B * H * A
+
+
+def tile_rwkvtimemix_pa_kernel(
+    tc, x, alpha, aa, bb, pp, time_decay, time_first, time_mix_k, time_mix_v, Wk, Wv,
+    out_0, out_1, out_2, out_3,
+):
+    nc = tc.nc
+    with ExitStack() as stack:
+        const = stack.enter_context(tc.tile_pool(name="const", bufs=1))
+        keep = stack.enter_context(tc.tile_pool(name="keep", bufs=1))
+        weights = stack.enter_context(tc.tile_pool(name="weights", bufs=4))
+        turned = stack.enter_context(tc.psum_pool(name="turned", bufs=4))
+        sums = stack.enter_context(tc.psum_pool(name="sums", bufs=2))
+
+        def rows_on_partitions(dram):
+            return dram.rearrange("(r p) n -> p r n", p=P)
+
+        def as_one_row(vector):
+            return vector.rearrange("(o c) -> o c", o=1)
+
+        def every_second_word(g, u):
+            return slice(g * PASS_WORDS + u, (g + 1) * PASS_WORDS, 2)
+
+        def channels(c):
+            return slice(c * N_TILE, (c + 1) * N_TILE)
+
+        mix_rows = const.tile([P, K_PASS], BF16)
+        nc.vector.memset(mix_rows[:], 0.0)
+        nc.scalar.dma_start(out=mix_rows[0:2, :], in_=time_mix_k.rearrange("(j c) -> j c", c=K_PASS))
+        nc.scalar.dma_start(out=mix_rows[2:4, :], in_=time_mix_v.rearrange("(j c) -> j c", c=K_PASS))
+        vec_rows = const.tile([P, 2 * A], BF16)
+        nc.vector.memset(vec_rows[:], 0.0)
+        nc.scalar.dma_start(out=vec_rows[0:1, 0:A], in_=as_one_row(time_first))
+        nc.scalar.dma_start(out=vec_rows[1:2, 0:A], in_=as_one_row(time_decay))
+        nc.scalar.dma_start(out=vec_rows[0:1, A : 2 * A], in_=as_one_row(time_decay))
+
+        identity = const.tile([P, P], F32)
+        make_identity(nc, identity[:])
+        ones = const.tile([P, P], BF16)
+        nc.vector.memset(ones[:], 1.0)
+        tiny = const.tile([P, 1], F32)
+        nc.vector.memset(tiny[:], TINY)
+        mix = const.tile([P, 2, 8], F32)
+        one_minus_mix = const.tile([P, 2, 8], F32)
+        first_plus_decay = const.tile([P, A], F32)
+        decay = const.tile([P, A], F32)
+
+        xk_words = keep.tile([P, PASSES, B], U32, align_bytes=64)
+        xk_scales = keep.tile([P, PASSES, B], U8, align_bytes=64)
+        xv_words = keep.tile([P, PASSES, B], U32, align_bytes=64)
+        xv_scales = keep.tile([P, PASSES, B], U8, align_bytes=64)
+        wk_words = keep.tile([P, COL_TILES, PASSES, N_TILE], U32, align_bytes=64)
+        wk_scales = keep.tile([P, COL_TILES, PASSES, N_TILE], U8, align_bytes=64)
+        wv_words = keep.tile([P, COL_TILES, PASSES, N_TILE], U32, align_bytes=64)
+        wv_scales = keep.tile([P, COL_TILES, PASSES, N_TILE], U8, align_bytes=64)
+
+        aa_sb = keep.tile([P, ROW_TILES, A], BF16)
+        bb_sb = keep.tile([P, ROW_TILES, A], BF16)
+        pp_sb = keep.tile([P, ROW_TILES, A], BF16)
+        log_shift = []
+        rho = []
+        decayed = []
+        for c in range(COL_TILES):
+            log_shift.append(keep.tile([P, ROW_TILES, N_TILE], F32, name="log_shift%d" % c))
+            rho.append(keep.tile([P, ROW_TILES, N_TILE], F32, name="rho%d" % c))
+            decayed.append(keep.tile([P, ROW_TILES, N_TILE], F32, name="decayed%d" % c))
+
+        def load_state_half(state_sb, state, c):
+            nc.sync.dma_start(out=state_sb[:, :, channels(c)], in_=rows_on_partitions(state)[:, :, channels(c)])
+
+        def load_weight_half(w, c):
+            w_sb = weights.tile([P, N_TILE // P, H], BF16, tag="w_sb")
+            nc.sync.dma_start(out=w_sb[:], in_=rows_on_partitions(w[channels(c), :]))
+            return w_sb
+
+        def quantise_weight_half(w_sb, words, scales, c):
+            for g in range(PASSES):
+                grouped = weights.tile([P, 4 * N_TILE], BF16, tag="w_grouped", bufs=2, align_bytes=64)
+                grouped_pairs = grouped[:].bitcast(F32).rearrange("p (a u) -> p a u", u=2)
+                for half in range(2):
+                    w_turned = turned.tile([P, 2, 2 * P], F32, tag="turned")
+                    for u in range(2):
+                        for i in range(2):
+                            block = w_sb[:, 2 * half + i, :].bitcast(F32)
+                            nc.tensor.transpose(
+                                w_turned[:, u, i * P : (i + 1) * P], block[:, every_second_word(g, u)], identity[:]
+                            )
+                    nc.scalar.copy(
+                        out=grouped_pairs[:, half * 2 * P : (half + 1) * 2 * P, :],
+                        in_=w_turned[:].rearrange("p u a -> p a u"),
+                    )
+                nc.vector.quantize_mx(
+                    out=words[:, c, g, :].bitcast(FP8X4), scales=scales[:, c, g, :], in_=grouped[:]
+                )
+
+        def logarithm_and_reciprocal_of_bb(c):
+            log_bb = keep.tile([P, ROW_TILES, N_TILE], F32, tag="log_bb")
+            nc.scalar.activation(out=log_bb[:], in_=bb_sb[:, :, channels(c)], func=ACT.Ln, bias=tiny[:])
+            nc.scalar.activation(out=rho[c][:], in_=log_bb[:], func=ACT.Exp, scale=-1.0)
+            return log_bb
+
+        def decay_pp(engine, c):
+            for r in range(ROW_TILES):
+                engine.tensor_tensor(
+                    out=decayed[c][:, r, :], in0=pp_sb[:, r, channels(c)], in1=decay[:, channels(c)], op=ALU.add
+                )
+
+        def shift_logarithm(engine, c, log_bb):
+            for r in range(ROW_TILES):
+                engine.tensor_tensor(
+                    out=log_shift[c][:, r, :], in0=log_bb[:, r, :], in1=first_plus_decay[:, channels(c)],
+                    op=ALU.subtract,
+                )
+
+        def old_average(engine, c):
+            for r in range(ROW_TILES):
+                engine.tensor_tensor(
+                    out=rho[c][:, r, :], in0=aa_sb[:, r, channels(c)], in1=rho[c][:, r, :], op=ALU.mult
+                )
+
+        with tc.tile_pool(name="front", bufs=1) as front:
+            x_sb = front.tile([P, ROW_TILES, H], BF16)
+            alpha_sb = front.tile([P, ROW_TILES, H], BF16)
+            load_state_half(bb_sb, bb, 0)
+            load_state_half(pp_sb, pp, 0)
+            for g in range(PASSES):
+                h_cols = slice(g * K_PASS, (g + 1) * K_PASS)
+                nc.sync.dma_start(out=x_sb[:, :, h_cols], in_=rows_on_partitions(x)[:, :, h_cols])
+                nc.sync.dma_start(out=alpha_sb[:, :, h_cols], in_=rows_on_partitions(alpha)[:, :, h_cols])
+            load_state_half(aa_sb, aa, 0)
+            wk_sb = [load_weight_half(Wk, 0)]
+            wv_sb = [load_weight_half(Wv, 0)]
+            load_state_half(bb_sb, bb, 1)
+            load_state_half(pp_sb, pp, 1)
+            load_state_half(aa_sb, aa, 1)
+            wk_sb.append(load_weight_half(Wk, 1))
+            wv_sb.append(load_weight_half(Wv, 1))
+
+            for c in range(COL_TILES):
+                for first_col, repeated in ((A, decay), (0, first_plus_decay)):
+                    repeated_ps = turned.tile([P, N_TILE], F32, tag="turned")
+                    nc.tensor.matmul(
+                        out=repeated_ps[:], lhsT=ones[:],
+                        rhs=vec_rows[:, first_col + c * N_TILE : first_col + (c + 1) * N_TILE], start=True, stop=True,
+                    )
+                    nc.vector.tensor_copy(out=repeated[:, channels(c)], in_=repeated_ps[:])
+
+            mix_turned = turned.tile([P, 2, P], F32, tag="turned")
+            for u in range(2):
+                nc.tensor.transpose(mix_turned[:, u, :], mix_rows[:].bitcast(F32)[:, every_second_word(0, u)], identity[:])
+            nc.vector.tensor_copy(out=mix[:], in_=mix_turned[:, :, 0:4].bitcast(BF16))
+            nc.vector.tensor_scalar(
+                out=one_minus_mix[:], in0=mix[:], scalar1=-1.0, scalar2=1.0, op0=ALU.mult, op1=ALU.add
+            )
+
+            log_bb = logarithm_and_reciprocal_of_bb(0)
+            decay_pp(nc.vector, 0)
+            shift_logarithm(nc.vector, 0, log_bb)
+            old_average(nc.gpsimd, 0)
+
+            xk_mixed = front.tile([P, PASSES, 4, B], BF16)
+            xv_mixed = front.tile([P, PASSES, 4, B], BF16)
+            for g, u in ((0, 0), (0, 1), (1, 0), (1, 1)):
+                x_turned = turned.tile([P, B], F32, tag="turned")
+                alpha_turned = turned.tile([P, B], F32, tag="turned")
+                for r in range(ROW_TILES):
+                    rows = slice(r * P, (r + 1) * P)
+                    words = every_second_word(g, u)
+                    nc.tensor.transpose(x_turned[:, rows], x_sb[:, r, :].bitcast(F32)[:, words], identity[:])
+                    nc.tensor.transpose(alpha_turned[:, rows], alpha_sb[:, r, :].bitcast(F32)[:, words], identity[:])
+                x_pairs = x_turned[:].bitcast(BF16).rearrange("p (b e) -> p b e", e=2)
+                alpha_pairs = alpha_turned[:].bitcast(BF16).rearrange("p (b e) -> p b e", e=2)
+                for e in range(2):
+                    for first_row, mixed in ((0, xk_mixed), (2, xv_mixed)):
+                        col = 2 * (first_row + g) + e
+                        alpha_part = front.tile([P, B], F32, tag="alpha_part", bufs=4)
+                        nc.scalar.activation(
+                            out=alpha_part[:], in_=alpha_pairs[:, :, e], func=ACT.Copy,
+                            scale=one_minus_mix[:, u, col : col + 1],
+                        )
+                        nc.vector.scalar_tensor_tensor(
+                            out=mixed[:, g, 2 * u + e, :], in0=x_pairs[:, :, e], scalar=mix[:, u, col : col + 1],
+                            in1=alpha_part[:], op0=ALU.mult, op1=ALU.add,
+                        )
+
+            xk_grouped = front.tile([P, PASSES, B, 4], BF16, align_bytes=64)
+            xv_grouped = front.tile([P, PASSES, B, 4], BF16, align_bytes=64)
+            for g in range(PASSES):
+                nc.vector.tensor_copy(
+                    out=xk_grouped[:, g].rearrange("p (c i) t -> p c t i", i=4),
+                    in_=xk_mixed[:, g].rearrange("p t (c i) -> p c t i", i=4),
+                )
+                nc.scalar.copy(
+                    out=xv_grouped[:, g].rearrange("p (c i) t -> p c t i", i=4),
+                    in_=xv_mixed[:, g].rearrange("p t (c i) -> p c t i", i=4),
+                )
+            for grouped, words, scales in ((xk_grouped, xk_words, xk_scales), (xv_grouped, xv_words, xv_scales)):
+                for g in range(PASSES):
+                    nc.vector.quantize_mx(
+                        out=words[:, g, :].bitcast(FP8X4), scales=scales[:, g, :],
+                        in_=grouped[:, g].rearrange("p b t -> p (b t)"),
+                    )
+
+        with tc.tile_pool(name="late", bufs=3) as late:
+
+            def project(c, r, x_words, x_scales, w_words, w_scales, tag):
+                acc = sums.tile([P, N_TILE], F32, tag=tag)
+                rows = slice(r * P, (r + 1) * P)
+                for g in range(PASSES):
+                    nc.tensor.matmul_mx(
+                        out=acc[:],
+                        lhsT=x_words[:, g, rows].bitcast(FP8X4), lhsT_scale=x_scales[:, g, rows],
+                        rhs=w_words[:, c, g, :].bitcast(FP8X4), rhs_scale=w_scales[:, c, g, :],
+                        start=(g == 0), stop=(g == PASSES - 1),
+                    )
+                return acc
+
+            def output_tile(c, r):
+                rows = slice(r * P, (r + 1) * P)
+                cols = channels(c)
+                k_ps = project(c, r, xk_words, xk_scales, wk_words, wk_scales, "k")
+                v_ps = project(c, r, xv_words, xv_scales, wv_words, wv_scales, "v")
+
+                d2 = late.tile([P, N_TILE], F32, tag="d2")
+                nc.vector.tensor_tensor(out=d2[:], in0=k_ps[:], in1=decayed[c][:, r, :], op=ALU.subtract)
+                qq2 = late.tile([P, N_TILE], F32, tag="qq2")
+                nc.vector.tensor_tensor(out=qq2[:], in0=k_ps[:], in1=decayed[c][:, r, :], op=ALU.max)
+                nc.sync.dma_start(out=out_3[rows, cols], in_=qq2[:])
+                wkv = late.tile([P, N_TILE], F32, tag="wkv")
+                nc.vector.tensor_tensor(out=wkv[:], in0=v_ps[:], in1=rho[c][:, r, :], op=ALU.subtract)
+                gate = late.tile([P, N_TILE], F32, tag="gate")
+                nc.vector.tensor_tensor(out=gate[:], in0=d2[:], in1=log_shift[c][:, r, :], op=ALU.subtract)
+
+                grow_old = late.tile([P, N_TILE], F32, tag="grow_old")
+                nc.scalar.activation(out=grow_old[:], in_=d2[:], func=ACT.Exp, scale=-1.0)
+                grow_new = late.tile([P, N_TILE], F32, tag="grow_new")
+                nc.scalar.activation(out=grow_new[:], in_=d2[:], func=ACT.Exp)
+                nc.scalar.activation(out=gate[:], in_=gate[:], func=ACT.Tanh, scale=0.5)
+
+                new_part = late.tile([P, N_TILE], F32, tag="new_part")
+                nc.vector.scalar_tensor_tensor(
+                    out=new_part[:], in0=grow_new[:], scalar=1.0, in1=v_ps[:], op0=ALU.min, op1=ALU.mult
+                )
+                next_aa = late.tile([P, N_TILE], F32, tag="next_aa")
+                nc.vector.scalar_tensor_tensor(
+                    out=next_aa[:], in0=grow_old[:], scalar=1.0, in1=aa_sb[:, r, cols], op0=ALU.min, op1=ALU.mult
+                )
+                next_bb = late.tile([P, N_TILE], F32, tag="next_bb")
+                nc.vector.scalar_tensor_tensor(
+                    out=next_bb[:], in0=grow_old[:], scalar=1.0, in1=bb_sb[:, r, cols], op0=ALU.min, op1=ALU.mult
+                )
+                nc.vector.scalar_tensor_tensor(
+                    out=wkv[:], in0=gate[:], scalar=1.0, in1=wkv[:], op0=ALU.add, op1=ALU.mult
+                )
+                nc.vector.tensor_tensor(out=next_aa[:], in0=next_aa[:], in1=new_part[:], op=ALU.add)
+                nc.sync.dma_start(out=out_1[rows, cols], in_=next_aa[:])
+                nc.vector.scalar_tensor_tensor(
+                    out=next_bb[:], in0=grow_new[:], scalar=1.0, in1=next_bb[:], op0=ALU.min, op1=ALU.add
+                )
+                nc.sync.dma_start(out=out_2[rows, cols], in_=next_bb[:])
+                nc.vector.scalar_tensor_tensor(
+                    out=wkv[:], in0=wkv[:], scalar=0.5, in1=rho[c][:, r, :], op0=ALU.mult, op1=ALU.add
+                )
+                nc.sync.dma_start(out=out_0[rows, cols], in_=wkv[:])
+
+            quantise_weight_half(wk_sb[0], wk_words, wk_scales, 0)
+            quantise_weight_half(wv_sb[0], wv_words, wv_scales, 0)
+            log_bb = logarithm_and_reciprocal_of_bb(1)
+            decay_pp(nc.gpsimd, 1)
+            shift_logarithm(nc.gpsimd, 1, log_bb)
+            old_average(nc.gpsimd, 1)
+            for r in range(ROW_TILES):
+                output_tile(0, r)
+                if r == ROW_TILES // 2 - 1:
+                    quantise_weight_half(wk_sb[1], wk_words, wk_scales, 1)
+                    quantise_weight_half(wv_sb[1], wv_words, wv_scales, 1)
+            for r in range(ROW_TILES):
+                output_tile(1, r)

@@ -1,3 +1,4 @@
+import math
 from contextlib import ExitStack
 
 import concourse.mybir as mybir
@@ -14,11 +15,17 @@ ACT = mybir.ActivationFunctionType
 B, H, A = 512, 1024, 1024
 P = 128
 ROW_TILES = B // P
+HALVES = 2
+HALF_TILES = ROW_TILES // HALVES
+HALF_ROWS = B // HALVES
 K_PASS = 4 * P
 PASSES = H // K_PASS
 N_TILE = 512
 COL_TILES = A // N_TILE
 PASS_WORDS = K_PASS // 2
+CH_BLOCKS = A // P
+BLOCKS_OF_TILE = N_TILE // P
+LN_HALF = math.log(0.5)
 TINY = 2.0 ** -60
 
 FLOPS = 2 * 2 * B * H * A
@@ -32,9 +39,12 @@ def tile_rwkvtimemix_pa_kernel(
     with ExitStack() as stack:
         const = stack.enter_context(tc.tile_pool(name="const", bufs=1))
         keep = stack.enter_context(tc.tile_pool(name="keep", bufs=1))
-        weights = stack.enter_context(tc.tile_pool(name="weights", bufs=4))
-        turned = stack.enter_context(tc.psum_pool(name="turned", bufs=4))
+        weights = stack.enter_context(tc.tile_pool(name="weights", bufs=3))
+        front = stack.enter_context(tc.tile_pool(name="front", bufs=1))
+        late = stack.enter_context(tc.tile_pool(name="late", bufs=2))
+        turned = stack.enter_context(tc.psum_pool(name="turned", bufs=3))
         sums = stack.enter_context(tc.psum_pool(name="sums", bufs=2))
+        shifts = stack.enter_context(tc.psum_pool(name="shifts", bufs=1))
 
         def rows_on_partitions(dram):
             return dram.rearrange("(r p) n -> p r n", p=P)
@@ -52,22 +62,23 @@ def tile_rwkvtimemix_pa_kernel(
         nc.vector.memset(mix_rows[:], 0.0)
         nc.scalar.dma_start(out=mix_rows[0:2, :], in_=time_mix_k.rearrange("(j c) -> j c", c=K_PASS))
         nc.scalar.dma_start(out=mix_rows[2:4, :], in_=time_mix_v.rearrange("(j c) -> j c", c=K_PASS))
-        vec_rows = const.tile([P, 2 * A], BF16)
+        vec_rows = const.tile([P, P], BF16)
         nc.vector.memset(vec_rows[:], 0.0)
-        nc.scalar.dma_start(out=vec_rows[0:1, 0:A], in_=as_one_row(time_first))
-        nc.scalar.dma_start(out=vec_rows[1:2, 0:A], in_=as_one_row(time_decay))
-        nc.scalar.dma_start(out=vec_rows[0:1, A : 2 * A], in_=as_one_row(time_decay))
+        nc.scalar.dma_start(out=vec_rows[0:CH_BLOCKS, :], in_=time_decay.rearrange("(j c) -> j c", c=P))
+        nc.scalar.dma_start(out=vec_rows[CH_BLOCKS : 2 * CH_BLOCKS, :], in_=time_first.rearrange("(j c) -> j c", c=P))
 
         identity = const.tile([P, P], F32)
         make_identity(nc, identity[:])
-        ones = const.tile([P, P], BF16)
-        nc.vector.memset(ones[:], 1.0)
+        identity_bf16 = const.tile([P, P], BF16)
+        nc.vector.tensor_copy(out=identity_bf16[:], in_=identity[:])
         tiny = const.tile([P, 1], F32)
         nc.vector.memset(tiny[:], TINY)
+        ln_half = const.tile([P, 1], F32)
+        nc.vector.tensor_scalar(out=ln_half[:], in0=tiny[:], scalar1=0.0, scalar2=LN_HALF, op0=ALU.mult, op1=ALU.add)
         mix = const.tile([P, 2, 8], F32)
         one_minus_mix = const.tile([P, 2, 8], F32)
-        first_plus_decay = const.tile([P, A], F32)
-        decay = const.tile([P, A], F32)
+        vec_cols = const.tile([P, 2 * CH_BLOCKS], F32)
+        minus_both = const.tile([P, CH_BLOCKS], F32)
 
         xk_words = keep.tile([P, PASSES, B], U32, align_bytes=64)
         xk_scales = keep.tile([P, PASSES, B], U8, align_bytes=64)
@@ -78,26 +89,58 @@ def tile_rwkvtimemix_pa_kernel(
         wv_words = keep.tile([P, COL_TILES, PASSES, N_TILE], U32, align_bytes=64)
         wv_scales = keep.tile([P, COL_TILES, PASSES, N_TILE], U8, align_bytes=64)
 
-        aa_sb = keep.tile([P, ROW_TILES, A], BF16)
-        bb_sb = keep.tile([P, ROW_TILES, A], BF16)
-        pp_sb = keep.tile([P, ROW_TILES, A], BF16)
-        log_shift = []
-        rho = []
+        log_bb = keep.tile([P, CH_BLOCKS, B], F32)
+        half_rho = []
         decayed = []
-        for c in range(COL_TILES):
-            log_shift.append(keep.tile([P, ROW_TILES, N_TILE], F32, name="log_shift%d" % c))
-            rho.append(keep.tile([P, ROW_TILES, N_TILE], F32, name="rho%d" % c))
-            decayed.append(keep.tile([P, ROW_TILES, N_TILE], F32, name="decayed%d" % c))
+        for half in range(HALVES):
+            half_rho.append(keep.tile([P, HALF_TILES, A], F32, name="half_rho%d" % half))
+            decayed.append(keep.tile([P, HALF_TILES, A], F32, name="decayed%d" % half))
 
-        def load_state_half(state_sb, state, c):
-            nc.sync.dma_start(out=state_sb[:, :, channels(c)], in_=rows_on_partitions(state)[:, :, channels(c)])
+        def half_rows(dram, half):
+            return rows_on_partitions(dram)[:, half * HALF_TILES : (half + 1) * HALF_TILES, :]
+
+        def load_rows(dram, half, tag, bufs):
+            rows_sb = keep.tile([P, HALF_TILES, dram.shape[1]], BF16, tag=tag, bufs=bufs)
+            nc.sync.dma_start(out=rows_sb[:], in_=half_rows(dram, half))
+            return rows_sb
 
         def load_weight_half(w, c):
             w_sb = weights.tile([P, N_TILE // P, H], BF16, tag="w_sb")
             nc.sync.dma_start(out=w_sb[:], in_=rows_on_partitions(w[channels(c), :]))
             return w_sb
 
-        def quantise_weight_half(w_sb, words, scales, c):
+        x_sb = [load_rows(x, 0, "x", 1)]
+        alpha_sb = [load_rows(alpha, 0, "alpha", 1)]
+        bb_sb = [load_rows(bb, 0, "bb", 2)]
+        bb_sb.append(load_rows(bb, 1, "bb", 2))
+        wk_sb = [load_weight_half(Wk, 0)]
+        pp_sb = [load_rows(pp, 0, "pp", 1)]
+        wv_sb = [load_weight_half(Wv, 0)]
+        aa_sb = [load_rows(aa, 0, "aa", 2)]
+        wk_sb.append(load_weight_half(Wk, 1))
+        wv_sb.append(load_weight_half(Wv, 1))
+        x_sb.append(load_rows(x, 1, "x", 1))
+        alpha_sb.append(load_rows(alpha, 1, "alpha", 1))
+        aa_sb.append(load_rows(aa, 1, "aa", 2))
+        pp_sb.append(load_rows(pp, 1, "pp", 1))
+
+        mix_turned = turned.tile([P, 2, P], F32, tag="turned")
+        for u in range(2):
+            nc.tensor.transpose(mix_turned[:, u, :], mix_rows[:].bitcast(F32)[:, every_second_word(0, u)], identity[:])
+        nc.vector.tensor_copy(out=mix[:], in_=mix_turned[:, :, 0:4].bitcast(BF16))
+        nc.vector.tensor_scalar(
+            out=one_minus_mix[:], in0=mix[:], scalar1=-1.0, scalar2=1.0, op0=ALU.mult, op1=ALU.add
+        )
+
+        vec_turned = turned.tile([P, P], BF16, tag="turned")
+        nc.tensor.transpose(vec_turned[:], vec_rows[:], identity_bf16[:])
+        nc.vector.tensor_copy(out=vec_cols[:], in_=vec_turned[:, 0 : 2 * CH_BLOCKS])
+        nc.vector.scalar_tensor_tensor(
+            out=minus_both[:], in0=vec_cols[:, 0:CH_BLOCKS], scalar=-1.0, in1=vec_cols[:, CH_BLOCKS : 2 * CH_BLOCKS],
+            op0=ALU.mult, op1=ALU.subtract,
+        )
+
+        def quantise_weight_half(w_sb, words, scales, c, copies):
             for g in range(PASSES):
                 grouped = weights.tile([P, 4 * N_TILE], BF16, tag="w_grouped", bufs=2, align_bytes=64)
                 grouped_pairs = grouped[:].bitcast(F32).rearrange("p (a u) -> p a u", u=2)
@@ -109,7 +152,7 @@ def tile_rwkvtimemix_pa_kernel(
                             nc.tensor.transpose(
                                 w_turned[:, u, i * P : (i + 1) * P], block[:, every_second_word(g, u)], identity[:]
                             )
-                    nc.scalar.copy(
+                    copies[half](
                         out=grouped_pairs[:, half * 2 * P : (half + 1) * 2 * P, :],
                         in_=w_turned[:].rearrange("p u a -> p a u"),
                     )
@@ -117,186 +160,210 @@ def tile_rwkvtimemix_pa_kernel(
                     out=words[:, c, g, :].bitcast(FP8X4), scales=scales[:, c, g, :], in_=grouped[:]
                 )
 
-        def logarithm_and_reciprocal_of_bb(c):
-            log_bb = keep.tile([P, ROW_TILES, N_TILE], F32, tag="log_bb")
-            nc.scalar.activation(out=log_bb[:], in_=bb_sb[:, :, channels(c)], func=ACT.Ln, bias=tiny[:])
-            nc.scalar.activation(out=rho[c][:], in_=log_bb[:], func=ACT.Exp, scale=-1.0)
-            return log_bb
-
-        def decay_pp(engine, c):
+        def logarithm_of_bb(j):
+            bb_turned = turned.tile([P, B], BF16, tag="turned")
             for r in range(ROW_TILES):
-                engine.tensor_tensor(
-                    out=decayed[c][:, r, :], in0=pp_sb[:, r, channels(c)], in1=decay[:, channels(c)], op=ALU.add
+                half, i = divmod(r, HALF_TILES)
+                nc.tensor.transpose(
+                    bb_turned[:, r * P : (r + 1) * P], bb_sb[half][:, i, j * P : (j + 1) * P], identity_bf16[:]
                 )
+            nc.scalar.activation(out=log_bb[:, j, :], in_=bb_turned[:], func=ACT.Ln, bias=tiny[:])
 
-        def shift_logarithm(engine, c, log_bb):
-            for r in range(ROW_TILES):
-                engine.tensor_tensor(
-                    out=log_shift[c][:, r, :], in0=log_bb[:, r, :], in1=first_plus_decay[:, channels(c)],
-                    op=ALU.subtract,
+        def spread(columns, j):
+            return columns[:, j : j + 1].to_broadcast([P, P])
+
+        def add_transposed(out, block, start, stop):
+            nc.tensor.matmul(out=out, lhsT=block, rhs=identity[:], start=start, stop=stop, is_transpose=True)
+
+        def decay_pp(half, i, c):
+            decayed_ps = turned.tile([P, N_TILE], F32, tag="turned")
+            for j in range(BLOCKS_OF_TILE):
+                block = slice(j * P, (j + 1) * P)
+                add_transposed(decayed_ps[:, block], spread(vec_cols, c * BLOCKS_OF_TILE + j), True, False)
+                nc.tensor.matmul(
+                    out=decayed_ps[:, block], lhsT=identity_bf16[:],
+                    rhs=pp_sb[half][:, i, c * N_TILE + j * P : c * N_TILE + (j + 1) * P], start=False, stop=True,
                 )
+            nc.scalar.copy(out=decayed[half][:, i, channels(c)], in_=decayed_ps[:])
 
-        def old_average(engine, c):
-            for r in range(ROW_TILES):
-                engine.tensor_tensor(
-                    out=rho[c][:, r, :], in0=aa_sb[:, r, channels(c)], in1=rho[c][:, r, :], op=ALU.mult
+        def log_rows(r, j):
+            return log_bb[:, j, r * P : (r + 1) * P]
+
+        def reciprocal_of_bb(half, i, c):
+            log_ps = turned.tile([P, N_TILE], F32, tag="turned")
+            for j in range(BLOCKS_OF_TILE):
+                nc.tensor.transpose(
+                    log_ps[:, j * P : (j + 1) * P], log_rows(half * HALF_TILES + i, c * BLOCKS_OF_TILE + j), identity[:]
                 )
-
-        with tc.tile_pool(name="front", bufs=1) as front:
-            x_sb = front.tile([P, ROW_TILES, H], BF16)
-            alpha_sb = front.tile([P, ROW_TILES, H], BF16)
-            load_state_half(bb_sb, bb, 0)
-            load_state_half(pp_sb, pp, 0)
-            for g in range(PASSES):
-                h_cols = slice(g * K_PASS, (g + 1) * K_PASS)
-                nc.sync.dma_start(out=x_sb[:, :, h_cols], in_=rows_on_partitions(x)[:, :, h_cols])
-                nc.sync.dma_start(out=alpha_sb[:, :, h_cols], in_=rows_on_partitions(alpha)[:, :, h_cols])
-            load_state_half(aa_sb, aa, 0)
-            wk_sb = [load_weight_half(Wk, 0)]
-            wv_sb = [load_weight_half(Wv, 0)]
-            load_state_half(bb_sb, bb, 1)
-            load_state_half(pp_sb, pp, 1)
-            load_state_half(aa_sb, aa, 1)
-            wk_sb.append(load_weight_half(Wk, 1))
-            wv_sb.append(load_weight_half(Wv, 1))
-
-            for c in range(COL_TILES):
-                for first_col, repeated in ((A, decay), (0, first_plus_decay)):
-                    repeated_ps = turned.tile([P, N_TILE], F32, tag="turned")
-                    nc.tensor.matmul(
-                        out=repeated_ps[:], lhsT=ones[:],
-                        rhs=vec_rows[:, first_col + c * N_TILE : first_col + (c + 1) * N_TILE], start=True, stop=True,
-                    )
-                    nc.vector.tensor_copy(out=repeated[:, channels(c)], in_=repeated_ps[:])
-
-            mix_turned = turned.tile([P, 2, P], F32, tag="turned")
-            for u in range(2):
-                nc.tensor.transpose(mix_turned[:, u, :], mix_rows[:].bitcast(F32)[:, every_second_word(0, u)], identity[:])
-            nc.vector.tensor_copy(out=mix[:], in_=mix_turned[:, :, 0:4].bitcast(BF16))
-            nc.vector.tensor_scalar(
-                out=one_minus_mix[:], in0=mix[:], scalar1=-1.0, scalar2=1.0, op0=ALU.mult, op1=ALU.add
+            nc.scalar.activation(
+                out=half_rho[half][:, i, channels(c)], in_=log_ps[:], func=ACT.Exp, scale=-1.0, bias=ln_half[:]
             )
 
-            log_bb = logarithm_and_reciprocal_of_bb(0)
-            decay_pp(nc.vector, 0)
-            shift_logarithm(nc.vector, 0, log_bb)
-            old_average(nc.gpsimd, 0)
+        def shifted_log(r, c):
+            shift_ps = shifts.tile([P, N_TILE], F32, tag="shift")
+            for j in range(BLOCKS_OF_TILE):
+                block = slice(j * P, (j + 1) * P)
+                add_transposed(shift_ps[:, block], log_rows(r, c * BLOCKS_OF_TILE + j), True, False)
+                add_transposed(shift_ps[:, block], spread(minus_both, c * BLOCKS_OF_TILE + j), False, True)
+            return shift_ps
 
-            xk_mixed = front.tile([P, PASSES, 4, B], BF16)
-            xv_mixed = front.tile([P, PASSES, 4, B], BF16)
-            for g, u in ((0, 0), (0, 1), (1, 0), (1, 1)):
-                x_turned = turned.tile([P, B], F32, tag="turned")
-                alpha_turned = turned.tile([P, B], F32, tag="turned")
-                for r in range(ROW_TILES):
-                    rows = slice(r * P, (r + 1) * P)
-                    words = every_second_word(g, u)
-                    nc.tensor.transpose(x_turned[:, rows], x_sb[:, r, :].bitcast(F32)[:, words], identity[:])
-                    nc.tensor.transpose(alpha_turned[:, rows], alpha_sb[:, r, :].bitcast(F32)[:, words], identity[:])
-                x_pairs = x_turned[:].bitcast(BF16).rearrange("p (b e) -> p b e", e=2)
-                alpha_pairs = alpha_turned[:].bitcast(BF16).rearrange("p (b e) -> p b e", e=2)
-                for e in range(2):
-                    for first_row, mixed in ((0, xk_mixed), (2, xv_mixed)):
-                        col = 2 * (first_row + g) + e
-                        alpha_part = front.tile([P, B], F32, tag="alpha_part", bufs=4)
-                        nc.scalar.activation(
-                            out=alpha_part[:], in_=alpha_pairs[:, :, e], func=ACT.Copy,
-                            scale=one_minus_mix[:, u, col : col + 1],
-                        )
-                        nc.vector.scalar_tensor_tensor(
-                            out=mixed[:, g, 2 * u + e, :], in0=x_pairs[:, :, e], scalar=mix[:, u, col : col + 1],
-                            in1=alpha_part[:], op0=ALU.mult, op1=ALU.add,
-                        )
+        def old_average(half, c):
+            for i in range(HALF_TILES):
+                nc.gpsimd.tensor_tensor(
+                    out=half_rho[half][:, i, channels(c)], in0=aa_sb[half][:, i, channels(c)],
+                    in1=half_rho[half][:, i, channels(c)], op=ALU.mult,
+                )
 
-            xk_grouped = front.tile([P, PASSES, B, 4], BF16, align_bytes=64)
-            xv_grouped = front.tile([P, PASSES, B, 4], BF16, align_bytes=64)
+        def regroup(engine_copy, mixed, grouped, g):
+            engine_copy(
+                out=grouped[:, g].rearrange("p (c i) t -> p c t i", i=4),
+                in_=mixed[:, g].rearrange("p t (c i) -> p c t i", i=4),
+            )
+
+        def mix_and_quantise(half, regroup_xk, regroup_xv):
+            xk_mixed = front.tile([P, PASSES, 4, HALF_ROWS], BF16, tag="xk_mixed")
+            xv_mixed = front.tile([P, PASSES, 4, HALF_ROWS], BF16, tag="xv_mixed")
+            xk_grouped = front.tile([P, PASSES, HALF_ROWS, 4], BF16, tag="xk_grouped", align_bytes=64)
+            xv_grouped = front.tile([P, PASSES, HALF_ROWS, 4], BF16, tag="xv_grouped", align_bytes=64)
             for g in range(PASSES):
-                nc.vector.tensor_copy(
-                    out=xk_grouped[:, g].rearrange("p (c i) t -> p c t i", i=4),
-                    in_=xk_mixed[:, g].rearrange("p t (c i) -> p c t i", i=4),
-                )
-                nc.scalar.copy(
-                    out=xv_grouped[:, g].rearrange("p (c i) t -> p c t i", i=4),
-                    in_=xv_mixed[:, g].rearrange("p t (c i) -> p c t i", i=4),
-                )
-            for grouped, words, scales in ((xk_grouped, xk_words, xk_scales), (xv_grouped, xv_words, xv_scales)):
-                for g in range(PASSES):
+                x_turned = turned.tile([P, 2, HALF_ROWS], F32, tag="turned")
+                alpha_turned = turned.tile([P, 2, HALF_ROWS], F32, tag="turned")
+                for act_turned, act_sb in ((x_turned, x_sb), (alpha_turned, alpha_sb)):
+                    for u in range(2):
+                        for i in range(HALF_TILES):
+                            block = act_sb[half][:, i, :].bitcast(F32)
+                            nc.tensor.transpose(
+                                act_turned[:, u, i * P : (i + 1) * P], block[:, every_second_word(g, u)], identity[:]
+                            )
+                for u in range(2):
+                    x_pairs = x_turned[:, u, :].bitcast(BF16).rearrange("p (b e) -> p b e", e=2)
+                    alpha_pairs = alpha_turned[:, u, :].bitcast(BF16).rearrange("p (b e) -> p b e", e=2)
+                    for e in range(2):
+                        for first_row, mixed in ((0, xk_mixed), (2, xv_mixed)):
+                            col = 2 * (first_row + g) + e
+                            alpha_part = front.tile([P, HALF_ROWS], F32, tag="alpha_part", bufs=6)
+                            nc.scalar.activation(
+                                out=alpha_part[:], in_=alpha_pairs[:, :, e], func=ACT.Copy,
+                                scale=one_minus_mix[:, u, col : col + 1],
+                            )
+                            nc.vector.scalar_tensor_tensor(
+                                out=mixed[:, g, 2 * u + e, :], in0=x_pairs[:, :, e], scalar=mix[:, u, col : col + 1],
+                                in1=alpha_part[:], op0=ALU.mult, op1=ALU.add,
+                            )
+                regroup(regroup_xk, xk_mixed, xk_grouped, g)
+                regroup(regroup_xv, xv_mixed, xv_grouped, g)
+            rows = slice(half * HALF_ROWS, (half + 1) * HALF_ROWS)
+            for g in range(PASSES):
+                for grouped, words, scales in ((xk_grouped, xk_words, xk_scales), (xv_grouped, xv_words, xv_scales)):
                     nc.vector.quantize_mx(
-                        out=words[:, g, :].bitcast(FP8X4), scales=scales[:, g, :],
+                        out=words[:, g, rows].bitcast(FP8X4), scales=scales[:, g, rows],
                         in_=grouped[:, g].rearrange("p b t -> p (b t)"),
                     )
 
-        with tc.tile_pool(name="late", bufs=3) as late:
-
-            def project(c, r, x_words, x_scales, w_words, w_scales, tag):
-                acc = sums.tile([P, N_TILE], F32, tag=tag)
-                rows = slice(r * P, (r + 1) * P)
-                for g in range(PASSES):
-                    nc.tensor.matmul_mx(
-                        out=acc[:],
-                        lhsT=x_words[:, g, rows].bitcast(FP8X4), lhsT_scale=x_scales[:, g, rows],
-                        rhs=w_words[:, c, g, :].bitcast(FP8X4), rhs_scale=w_scales[:, c, g, :],
-                        start=(g == 0), stop=(g == PASSES - 1),
-                    )
-                return acc
-
-            def output_tile(c, r):
-                rows = slice(r * P, (r + 1) * P)
-                cols = channels(c)
-                k_ps = project(c, r, xk_words, xk_scales, wk_words, wk_scales, "k")
-                v_ps = project(c, r, xv_words, xv_scales, wv_words, wv_scales, "v")
-
-                d2 = late.tile([P, N_TILE], F32, tag="d2")
-                nc.vector.tensor_tensor(out=d2[:], in0=k_ps[:], in1=decayed[c][:, r, :], op=ALU.subtract)
-                qq2 = late.tile([P, N_TILE], F32, tag="qq2")
-                nc.vector.tensor_tensor(out=qq2[:], in0=k_ps[:], in1=decayed[c][:, r, :], op=ALU.max)
-                nc.sync.dma_start(out=out_3[rows, cols], in_=qq2[:])
-                wkv = late.tile([P, N_TILE], F32, tag="wkv")
-                nc.vector.tensor_tensor(out=wkv[:], in0=v_ps[:], in1=rho[c][:, r, :], op=ALU.subtract)
-                gate = late.tile([P, N_TILE], F32, tag="gate")
-                nc.vector.tensor_tensor(out=gate[:], in0=d2[:], in1=log_shift[c][:, r, :], op=ALU.subtract)
-
-                grow_old = late.tile([P, N_TILE], F32, tag="grow_old")
-                nc.scalar.activation(out=grow_old[:], in_=d2[:], func=ACT.Exp, scale=-1.0)
-                grow_new = late.tile([P, N_TILE], F32, tag="grow_new")
-                nc.scalar.activation(out=grow_new[:], in_=d2[:], func=ACT.Exp)
-                nc.scalar.activation(out=gate[:], in_=gate[:], func=ACT.Tanh, scale=0.5)
-
-                new_part = late.tile([P, N_TILE], F32, tag="new_part")
-                nc.vector.scalar_tensor_tensor(
-                    out=new_part[:], in0=grow_new[:], scalar=1.0, in1=v_ps[:], op0=ALU.min, op1=ALU.mult
+        def project(c, r, x_words, x_scales, w_words, w_scales, tag):
+            acc = sums.tile([P, N_TILE], F32, tag=tag)
+            rows = slice(r * P, (r + 1) * P)
+            for g in range(PASSES):
+                nc.tensor.matmul_mx(
+                    out=acc[:],
+                    lhsT=x_words[:, g, rows].bitcast(FP8X4), lhsT_scale=x_scales[:, g, rows],
+                    rhs=w_words[:, c, g, :].bitcast(FP8X4), rhs_scale=w_scales[:, c, g, :],
+                    start=(g == 0), stop=(g == PASSES - 1),
                 )
-                next_aa = late.tile([P, N_TILE], F32, tag="next_aa")
-                nc.vector.scalar_tensor_tensor(
-                    out=next_aa[:], in0=grow_old[:], scalar=1.0, in1=aa_sb[:, r, cols], op0=ALU.min, op1=ALU.mult
-                )
-                next_bb = late.tile([P, N_TILE], F32, tag="next_bb")
-                nc.vector.scalar_tensor_tensor(
-                    out=next_bb[:], in0=grow_old[:], scalar=1.0, in1=bb_sb[:, r, cols], op0=ALU.min, op1=ALU.mult
-                )
-                nc.vector.scalar_tensor_tensor(
-                    out=wkv[:], in0=gate[:], scalar=1.0, in1=wkv[:], op0=ALU.add, op1=ALU.mult
-                )
-                nc.vector.tensor_tensor(out=next_aa[:], in0=next_aa[:], in1=new_part[:], op=ALU.add)
-                nc.sync.dma_start(out=out_1[rows, cols], in_=next_aa[:])
-                nc.vector.scalar_tensor_tensor(
-                    out=next_bb[:], in0=grow_new[:], scalar=1.0, in1=next_bb[:], op0=ALU.min, op1=ALU.add
-                )
-                nc.sync.dma_start(out=out_2[rows, cols], in_=next_bb[:])
-                nc.vector.scalar_tensor_tensor(
-                    out=wkv[:], in0=wkv[:], scalar=0.5, in1=rho[c][:, r, :], op0=ALU.mult, op1=ALU.add
-                )
-                nc.sync.dma_start(out=out_0[rows, cols], in_=wkv[:])
+            return acc
 
-            quantise_weight_half(wk_sb[0], wk_words, wk_scales, 0)
-            quantise_weight_half(wv_sb[0], wv_words, wv_scales, 0)
-            log_bb = logarithm_and_reciprocal_of_bb(1)
-            decay_pp(nc.gpsimd, 1)
-            shift_logarithm(nc.gpsimd, 1, log_bb)
-            old_average(nc.gpsimd, 1)
-            for r in range(ROW_TILES):
-                output_tile(0, r)
-                if r == ROW_TILES // 2 - 1:
-                    quantise_weight_half(wk_sb[1], wk_words, wk_scales, 1)
-                    quantise_weight_half(wv_sb[1], wv_words, wv_scales, 1)
-            for r in range(ROW_TILES):
-                output_tile(1, r)
+        def output_pair(half, c, helper):
+            cols = channels(c)
+            tiles = range(HALF_TILES)
+            k_ps = []
+            v_ps = []
+            for i in tiles:
+                k_ps.append(project(c, half * HALF_TILES + i, xk_words, xk_scales, wk_words, wk_scales, "k"))
+            for i in tiles:
+                v_ps.append(project(c, half * HALF_TILES + i, xv_words, xv_scales, wv_words, wv_scales, "v"))
+            decayed_tiles = decayed[half][:, :, cols]
+
+            def pair_tile(tag):
+                pair = late.tile([P, HALF_TILES, N_TILE], F32, tag=tag)
+                return pair
+
+            d2 = pair_tile("d2")
+            gate = pair_tile("gate")
+            qq2 = pair_tile("qq2")
+            for i in tiles:
+                nc.vector.tensor_tensor(out=d2[:, i, :], in0=k_ps[i][:], in1=decayed_tiles[:, i, :], op=ALU.subtract)
+            for i in tiles:
+                shift_ps = shifted_log(half * HALF_TILES + i, c)
+                nc.vector.tensor_tensor(out=gate[:, i, :], in0=d2[:, i, :], in1=shift_ps[:], op=ALU.subtract)
+                nc.vector.tensor_tensor(out=qq2[:, i, :], in0=k_ps[i][:], in1=decayed_tiles[:, i, :], op=ALU.max)
+            nc.sync.dma_start(out=half_rows(out_3, half)[:, :, cols], in_=qq2[:])
+            swing = pair_tile("swing")
+            wkv = pair_tile("wkv")
+            for i in tiles:
+                nc.vector.scalar_tensor_tensor(
+                    out=swing[:, i, :], in0=v_ps[i][:], scalar=0.5, in1=half_rho[half][:, i, cols],
+                    op0=ALU.mult, op1=ALU.subtract,
+                )
+            for i in tiles:
+                nc.vector.scalar_tensor_tensor(
+                    out=wkv[:, i, :], in0=v_ps[i][:], scalar=0.5, in1=half_rho[half][:, i, cols],
+                    op0=ALU.mult, op1=ALU.add,
+                )
+
+            grow_old = pair_tile("grow_old")
+            nc.scalar.activation(out=grow_old[:], in_=d2[:], func=ACT.Exp, scale=-1.0)
+            grow_new = d2
+            nc.scalar.activation(out=grow_new[:], in_=d2[:], func=ACT.Exp)
+            nc.scalar.activation(out=gate[:], in_=gate[:], func=ACT.Tanh, scale=0.5)
+
+            new_part = pair_tile("new_part")
+            for i in tiles:
+                nc.vector.scalar_tensor_tensor(
+                    out=new_part[:, i, :], in0=grow_new[:, i, :], scalar=1.0, in1=v_ps[i][:], op0=ALU.min, op1=ALU.mult
+                )
+            next_aa = pair_tile("next_aa")
+            nc.vector.scalar_tensor_tensor(
+                out=next_aa[:], in0=grow_old[:], scalar=1.0, in1=aa_sb[half][:, :, cols], op0=ALU.min, op1=ALU.mult
+            )
+            next_bb = grow_old
+            nc.vector.scalar_tensor_tensor(
+                out=next_bb[:], in0=grow_old[:], scalar=1.0, in1=bb_sb[half][:, :, cols], op0=ALU.min, op1=ALU.mult
+            )
+            nc.vector.scalar_tensor_tensor(
+                out=next_bb[:], in0=grow_new[:], scalar=1.0, in1=next_bb[:], op0=ALU.min, op1=ALU.add
+            )
+            nc.sync.dma_start(out=half_rows(out_2, half)[:, :, cols], in_=next_bb[:])
+            for i in tiles:
+                helper.tensor_tensor(out=swing[:, i, :], in0=gate[:, i, :], in1=swing[:, i, :], op=ALU.mult)
+            for i in tiles:
+                helper.tensor_tensor(out=wkv[:, i, :], in0=wkv[:, i, :], in1=swing[:, i, :], op=ALU.add)
+            nc.sync.dma_start(out=half_rows(out_0, half)[:, :, cols], in_=wkv[:])
+            for i in tiles:
+                helper.tensor_tensor(out=next_aa[:, i, :], in0=next_aa[:, i, :], in1=new_part[:, i, :], op=ALU.add)
+            nc.sync.dma_start(out=half_rows(out_1, half)[:, :, cols], in_=next_aa[:])
+
+        def prepare_state(half, c):
+            for i in range(HALF_TILES):
+                decay_pp(half, i, c)
+            for i in range(HALF_TILES):
+                reciprocal_of_bb(half, i, c)
+            old_average(half, c)
+
+        both = (nc.scalar.copy, nc.vector.tensor_copy)
+        scalar_alone = (nc.scalar.copy, nc.scalar.copy)
+        mix_and_quantise(0, nc.vector.tensor_copy, nc.scalar.copy)
+        for j in range(CH_BLOCKS):
+            logarithm_of_bb(j)
+        prepare_state(0, 0)
+        quantise_weight_half(wk_sb[0], wk_words, wk_scales, 0, both)
+        quantise_weight_half(wv_sb[0], wv_words, wv_scales, 0, both)
+        output_pair(0, 0, nc.gpsimd)
+        quantise_weight_half(wk_sb[1], wk_words, wk_scales, 1, scalar_alone)
+        quantise_weight_half(wv_sb[1], wv_words, wv_scales, 1, scalar_alone)
+        prepare_state(0, 1)
+        mix_and_quantise(1, nc.scalar.copy, nc.scalar.copy)
+        prepare_state(1, 0)
+        output_pair(0, 1, nc.gpsimd)
+        prepare_state(1, 1)
+        output_pair(1, 0, nc.gpsimd)
+        output_pair(1, 1, nc.vector)

@@ -357,13 +357,13 @@ def tile_rwkvtimemix_pa_kernel(
         prepare_state(0, 0)
         quantise_weight_half(wk_sb[0], wk_words, wk_scales, 0, both)
         quantise_weight_half(wv_sb[0], wv_words, wv_scales, 0, both)
-        output_pair(0, 0, nc.gpsimd)
+        output_pair(0, 0, nc.vector)
         quantise_weight_half(wk_sb[1], wk_words, wk_scales, 1, scalar_alone)
         quantise_weight_half(wv_sb[1], wv_words, wv_scales, 1, scalar_alone)
         prepare_state(0, 1)
         mix_and_quantise(1, nc.scalar.copy, nc.scalar.copy)
         prepare_state(1, 0)
-        output_pair(0, 1, nc.gpsimd)
+        output_pair(0, 1, nc.vector)
         prepare_state(1, 1)
-        output_pair(1, 0, nc.gpsimd)
+        output_pair(1, 0, nc.vector)
         output_pair(1, 1, nc.vector)

@@ -15,16 +15,14 @@ ACT = mybir.ActivationFunctionType
 B, H, A = 512, 1024, 1024
 P = 128
 ROW_TILES = B // P
-HALVES = 2
-HALF_TILES = ROW_TILES // HALVES
-HALF_ROWS = B // HALVES
+PAIRS = ROW_TILES // 2
 K_PASS = 4 * P
 PASSES = H // K_PASS
-N_TILE = 512
-COL_TILES = A // N_TILE
 PASS_WORDS = K_PASS // 2
-CH_BLOCKS = A // P
-BLOCKS_OF_TILE = N_TILE // P
+COLS = 256
+COL_BLOCKS = A // COLS
+CH_TILES = A // P
+TILES_OF_BLOCK = COLS // P
 LN_HALF = math.log(0.5)
 TINY = 2.0 ** -60
 
@@ -39,92 +37,73 @@ def tile_rwkvtimemix_pa_kernel(
     with ExitStack() as stack:
         const = stack.enter_context(tc.tile_pool(name="const", bufs=1))
         keep = stack.enter_context(tc.tile_pool(name="keep", bufs=1))
-        weights = stack.enter_context(tc.tile_pool(name="weights", bufs=3))
+        flow = stack.enter_context(tc.tile_pool(name="flow", bufs=2))
         front = stack.enter_context(tc.tile_pool(name="front", bufs=1))
         late = stack.enter_context(tc.tile_pool(name="late", bufs=2))
-        turned = stack.enter_context(tc.psum_pool(name="turned", bufs=3))
-        sums = stack.enter_context(tc.psum_pool(name="sums", bufs=2))
-        shifts = stack.enter_context(tc.psum_pool(name="shifts", bufs=1))
+        banks = stack.enter_context(tc.psum_pool(name="banks", bufs=2))
 
         def rows_on_partitions(dram):
             return dram.rearrange("(r p) n -> p r n", p=P)
-
-        def as_one_row(vector):
-            return vector.rearrange("(o c) -> o c", o=1)
 
         def every_second_word(g, u):
             return slice(g * PASS_WORDS + u, (g + 1) * PASS_WORDS, 2)
 
         def channels(c):
-            return slice(c * N_TILE, (c + 1) * N_TILE)
+            return slice(c * COLS, (c + 1) * COLS)
 
         mix_rows = const.tile([P, K_PASS], BF16)
-        nc.vector.memset(mix_rows[:], 0.0)
-        nc.scalar.dma_start(out=mix_rows[0:2, :], in_=time_mix_k.rearrange("(j c) -> j c", c=K_PASS))
-        nc.scalar.dma_start(out=mix_rows[2:4, :], in_=time_mix_v.rearrange("(j c) -> j c", c=K_PASS))
+        nc.gpsimd.memset(mix_rows[:], 0.0)
         vec_rows = const.tile([P, P], BF16)
-        nc.vector.memset(vec_rows[:], 0.0)
-        nc.scalar.dma_start(out=vec_rows[0:CH_BLOCKS, :], in_=time_decay.rearrange("(j c) -> j c", c=P))
-        nc.scalar.dma_start(out=vec_rows[CH_BLOCKS : 2 * CH_BLOCKS, :], in_=time_first.rearrange("(j c) -> j c", c=P))
+        nc.gpsimd.memset(vec_rows[:], 0.0)
+        nc.sync.dma_start(out=mix_rows[0:2, :], in_=time_mix_k.rearrange("(j c) -> j c", c=K_PASS))
+        nc.sync.dma_start(out=mix_rows[2:4, :], in_=time_mix_v.rearrange("(j c) -> j c", c=K_PASS))
+        x_sb = keep.tile([P, ROW_TILES, H], BF16)
+        alpha_sb = keep.tile([P, ROW_TILES, H], BF16)
+        nc.sync.dma_start(out=vec_rows[0:CH_TILES, :], in_=time_decay.rearrange("(j c) -> j c", c=P))
+        nc.sync.dma_start(out=vec_rows[CH_TILES : 2 * CH_TILES, :], in_=time_first.rearrange("(j c) -> j c", c=P))
+        for g in range(PASSES):
+            h_cols = slice(g * K_PASS, (g + 1) * K_PASS)
+            nc.sync.dma_start(out=x_sb[:, :, h_cols], in_=rows_on_partitions(x)[:, :, h_cols])
+            nc.sync.dma_start(out=alpha_sb[:, :, h_cols], in_=rows_on_partitions(alpha)[:, :, h_cols])
 
+        def load_state(state, name):
+            state_sb = keep.tile([P, ROW_TILES, A], BF16, name=name)
+            nc.sync.dma_start(out=state_sb[:], in_=rows_on_partitions(state))
+            return state_sb
+
+        def load_weights(w, c, tag):
+            w_sb = flow.tile([P, TILES_OF_BLOCK, H], BF16, tag=tag)
+            nc.sync.dma_start(out=w_sb[:], in_=w[channels(c), :].rearrange("(i p) n -> p i n", p=P))
+            return w_sb
+
+        bb_sb = load_state(bb, "bb_sb")
+        wk_sb = [load_weights(Wk, 0, "wk")]
+        wv_sb = [load_weights(Wv, 0, "wv")]
+        pp_sb = load_state(pp, "pp_sb")
+        aa_sb = load_state(aa, "aa_sb")
+        for c in range(1, COL_BLOCKS):
+            wk_sb.append(load_weights(Wk, c, "wk"))
+            wv_sb.append(load_weights(Wv, c, "wv"))
+
+        tiny = const.tile([P, 1], F32)
+        nc.vector.memset(tiny[:], TINY)
+        warm = const.tile([P, 1], F32)
+        nc.scalar.activation(out=warm[:], in_=tiny[:], func=ACT.Ln)
+        ln_half = const.tile([P, 1], F32)
+        nc.vector.tensor_scalar(out=ln_half[:], in0=tiny[:], scalar1=0.0, scalar2=LN_HALF, op0=ALU.mult, op1=ALU.add)
         identity = const.tile([P, P], F32)
         make_identity(nc, identity[:])
         identity_bf16 = const.tile([P, P], BF16)
         nc.vector.tensor_copy(out=identity_bf16[:], in_=identity[:])
-        tiny = const.tile([P, 1], F32)
-        nc.vector.memset(tiny[:], TINY)
-        ln_half = const.tile([P, 1], F32)
-        nc.vector.tensor_scalar(out=ln_half[:], in0=tiny[:], scalar1=0.0, scalar2=LN_HALF, op0=ALU.mult, op1=ALU.add)
         mix = const.tile([P, 2, 8], F32)
         one_minus_mix = const.tile([P, 2, 8], F32)
-        vec_cols = const.tile([P, 2 * CH_BLOCKS], F32)
-        minus_both = const.tile([P, CH_BLOCKS], F32)
+        vec_cols = const.tile([P, 2 * CH_TILES], F32)
+        minus_both = const.tile([P, CH_TILES], F32)
 
-        xk_words = keep.tile([P, PASSES, B], U32, align_bytes=64)
-        xk_scales = keep.tile([P, PASSES, B], U8, align_bytes=64)
-        xv_words = keep.tile([P, PASSES, B], U32, align_bytes=64)
-        xv_scales = keep.tile([P, PASSES, B], U8, align_bytes=64)
-        wk_words = keep.tile([P, COL_TILES, PASSES, N_TILE], U32, align_bytes=64)
-        wk_scales = keep.tile([P, COL_TILES, PASSES, N_TILE], U8, align_bytes=64)
-        wv_words = keep.tile([P, COL_TILES, PASSES, N_TILE], U32, align_bytes=64)
-        wv_scales = keep.tile([P, COL_TILES, PASSES, N_TILE], U8, align_bytes=64)
+        order_kept = {mybir.EngineType.DVE, mybir.EngineType.Pool, mybir.EngineType.Activation}
+        stack.enter_context(tc.manual_schedule(engines=order_kept))
 
-        log_bb = keep.tile([P, CH_BLOCKS, B], F32)
-        half_rho = []
-        decayed = []
-        for half in range(HALVES):
-            half_rho.append(keep.tile([P, HALF_TILES, A], F32, name="half_rho%d" % half))
-            decayed.append(keep.tile([P, HALF_TILES, A], F32, name="decayed%d" % half))
-
-        def half_rows(dram, half):
-            return rows_on_partitions(dram)[:, half * HALF_TILES : (half + 1) * HALF_TILES, :]
-
-        def load_rows(dram, half, tag, bufs):
-            rows_sb = keep.tile([P, HALF_TILES, dram.shape[1]], BF16, tag=tag, bufs=bufs)
-            nc.sync.dma_start(out=rows_sb[:], in_=half_rows(dram, half))
-            return rows_sb
-
-        def load_weight_half(w, c):
-            w_sb = weights.tile([P, N_TILE // P, H], BF16, tag="w_sb")
-            nc.sync.dma_start(out=w_sb[:], in_=rows_on_partitions(w[channels(c), :]))
-            return w_sb
-
-        x_sb = [load_rows(x, 0, "x", 1)]
-        alpha_sb = [load_rows(alpha, 0, "alpha", 1)]
-        bb_sb = [load_rows(bb, 0, "bb", 2)]
-        bb_sb.append(load_rows(bb, 1, "bb", 2))
-        wk_sb = [load_weight_half(Wk, 0)]
-        pp_sb = [load_rows(pp, 0, "pp", 1)]
-        wv_sb = [load_weight_half(Wv, 0)]
-        aa_sb = [load_rows(aa, 0, "aa", 2)]
-        wk_sb.append(load_weight_half(Wk, 1))
-        wv_sb.append(load_weight_half(Wv, 1))
-        x_sb.append(load_rows(x, 1, "x", 1))
-        alpha_sb.append(load_rows(alpha, 1, "alpha", 1))
-        aa_sb.append(load_rows(aa, 1, "aa", 2))
-        pp_sb.append(load_rows(pp, 1, "pp", 1))
-
-        mix_turned = turned.tile([P, 2, P], F32, tag="turned")
+        mix_turned = banks.tile([P, 2, P], F32, tag="turned")
         for u in range(2):
             nc.tensor.transpose(mix_turned[:, u, :], mix_rows[:].bitcast(F32)[:, every_second_word(0, u)], identity[:])
         nc.vector.tensor_copy(out=mix[:], in_=mix_turned[:, :, 0:4].bitcast(BF16))
@@ -132,42 +111,66 @@ def tile_rwkvtimemix_pa_kernel(
             out=one_minus_mix[:], in0=mix[:], scalar1=-1.0, scalar2=1.0, op0=ALU.mult, op1=ALU.add
         )
 
-        vec_turned = turned.tile([P, P], BF16, tag="turned")
+        vec_turned = banks.tile([P, P], BF16, tag="turned")
         nc.tensor.transpose(vec_turned[:], vec_rows[:], identity_bf16[:])
-        nc.vector.tensor_copy(out=vec_cols[:], in_=vec_turned[:, 0 : 2 * CH_BLOCKS])
+        nc.vector.tensor_copy(out=vec_cols[:], in_=vec_turned[:, 0 : 2 * CH_TILES])
         nc.vector.scalar_tensor_tensor(
-            out=minus_both[:], in0=vec_cols[:, 0:CH_BLOCKS], scalar=-1.0, in1=vec_cols[:, CH_BLOCKS : 2 * CH_BLOCKS],
+            out=minus_both[:], in0=vec_cols[:, 0:CH_TILES], scalar=-1.0, in1=vec_cols[:, CH_TILES : 2 * CH_TILES],
             op0=ALU.mult, op1=ALU.subtract,
         )
 
-        def quantise_weight_half(w_sb, words, scales, c, copies):
+        xk_words = keep.tile([P, PASSES, B], U32, align_bytes=64)
+        xk_scales = keep.tile([P, PASSES, B], U8, align_bytes=64)
+        xv_words = keep.tile([P, PASSES, B], U32, align_bytes=64)
+        xv_scales = keep.tile([P, PASSES, B], U8, align_bytes=64)
+
+        def regroup(copy, mixed, grouped, g):
+            copy(
+                out=grouped[:, g].rearrange("p (c i) t -> p c t i", i=4),
+                in_=mixed[:, g].rearrange("p t (c i) -> p c t i", i=4),
+            )
+
+        xk_mixed = front.tile([P, PASSES, 4, B], BF16)
+        xv_mixed = front.tile([P, PASSES, 4, B], BF16)
+        xk_grouped = front.tile([P, PASSES, B, 4], BF16, align_bytes=64)
+        xv_grouped = front.tile([P, PASSES, B, 4], BF16, align_bytes=64)
+        for g in range(PASSES):
+            for u in range(2):
+                x_turned = banks.tile([P, B], F32, tag="k")
+                alpha_turned = banks.tile([P, B], F32, tag="v")
+                for act_turned, act_sb in ((alpha_turned, alpha_sb), (x_turned, x_sb)):
+                    for r in range(ROW_TILES):
+                        nc.tensor.transpose(
+                            act_turned[:, r * P : (r + 1) * P],
+                            act_sb[:, r, :].bitcast(F32)[:, every_second_word(g, u)], identity[:],
+                        )
+                x_pairs = x_turned[:].bitcast(BF16).rearrange("p (b e) -> p b e", e=2)
+                alpha_pairs = alpha_turned[:].bitcast(BF16).rearrange("p (b e) -> p b e", e=2)
+                for e in range(2):
+                    for first_row, mixed in ((0, xk_mixed), (2, xv_mixed)):
+                        col = 2 * (first_row + g) + e
+                        alpha_part = front.tile([P, B], F32, tag="alpha_part", bufs=4)
+                        nc.scalar.activation(
+                            out=alpha_part[:], in_=alpha_pairs[:, :, e], func=ACT.Copy,
+                            scale=one_minus_mix[:, u, col : col + 1],
+                        )
+                        nc.vector.scalar_tensor_tensor(
+                            out=mixed[:, g, 2 * u + e, :], in0=x_pairs[:, :, e], scalar=mix[:, u, col : col + 1],
+                            in1=alpha_part[:], op0=ALU.mult, op1=ALU.add,
+                        )
+            regroup(nc.vector.tensor_copy, xk_mixed, xk_grouped, g)
+            regroup(nc.vector.tensor_copy, xv_mixed, xv_grouped, g)
+        for grouped, words, scales in ((xk_grouped, xk_words, xk_scales), (xv_grouped, xv_words, xv_scales)):
             for g in range(PASSES):
-                grouped = weights.tile([P, 4 * N_TILE], BF16, tag="w_grouped", bufs=2, align_bytes=64)
-                grouped_pairs = grouped[:].bitcast(F32).rearrange("p (a u) -> p a u", u=2)
-                for half in range(2):
-                    w_turned = turned.tile([P, 2, 2 * P], F32, tag="turned")
-                    for u in range(2):
-                        for i in range(2):
-                            block = w_sb[:, 2 * half + i, :].bitcast(F32)
-                            nc.tensor.transpose(
-                                w_turned[:, u, i * P : (i + 1) * P], block[:, every_second_word(g, u)], identity[:]
-                            )
-                    copies[half](
-                        out=grouped_pairs[:, half * 2 * P : (half + 1) * 2 * P, :],
-                        in_=w_turned[:].rearrange("p u a -> p a u"),
-                    )
                 nc.vector.quantize_mx(
-                    out=words[:, c, g, :].bitcast(FP8X4), scales=scales[:, c, g, :], in_=grouped[:]
+                    out=words[:, g, :].bitcast(FP8X4), scales=scales[:, g, :],
+                    in_=grouped[:, g].rearrange("p b t -> p (b t)"),
                 )
 
-        def logarithm_of_bb(j):
-            bb_turned = turned.tile([P, B], BF16, tag="turned")
-            for r in range(ROW_TILES):
-                half, i = divmod(r, HALF_TILES)
-                nc.tensor.transpose(
-                    bb_turned[:, r * P : (r + 1) * P], bb_sb[half][:, i, j * P : (j + 1) * P], identity_bf16[:]
-                )
-            nc.scalar.activation(out=log_bb[:, j, :], in_=bb_turned[:], func=ACT.Ln, bias=tiny[:])
+        log_bb = keep.tile([P, CH_TILES, B], F32)
+
+        def log_rows(r, j):
+            return log_bb[:, j, r * P : (r + 1) * P]
 
         def spread(columns, j):
             return columns[:, j : j + 1].to_broadcast([P, P])
@@ -175,195 +178,206 @@ def tile_rwkvtimemix_pa_kernel(
         def add_transposed(out, block, start, stop):
             nc.tensor.matmul(out=out, lhsT=block, rhs=identity[:], start=start, stop=stop, is_transpose=True)
 
-        def decay_pp(half, i, c):
-            decayed_ps = turned.tile([P, N_TILE], F32, tag="turned")
-            for j in range(BLOCKS_OF_TILE):
-                block = slice(j * P, (j + 1) * P)
-                add_transposed(decayed_ps[:, block], spread(vec_cols, c * BLOCKS_OF_TILE + j), True, False)
-                nc.tensor.matmul(
-                    out=decayed_ps[:, block], lhsT=identity_bf16[:],
-                    rhs=pp_sb[half][:, i, c * N_TILE + j * P : c * N_TILE + (j + 1) * P], start=False, stop=True,
+        def parts(bank, c, pair):
+            return [
+                (2 * pair + i, c * TILES_OF_BLOCK + j, bank[:, i, j * P : (j + 1) * P])
+                for i in range(2)
+                for j in range(TILES_OF_BLOCK)
+            ]
+
+        def pair_rows(pair):
+            return slice(2 * pair, 2 * pair + 2)
+
+        def prepare_state(c):
+            half_rho = flow.tile([P, ROW_TILES, COLS], F32, tag="half_rho")
+            decayed = flow.tile([P, ROW_TILES, COLS], F32, tag="decayed")
+            for pair in range(PAIRS):
+                log_ps = banks.tile([P, 2, COLS], F32, tag="turned")
+                for r, j, part in parts(log_ps, c, pair):
+                    nc.tensor.transpose(part, log_rows(r, j), identity[:])
+                nc.scalar.activation(
+                    out=half_rho[:, pair_rows(pair), :], in_=log_ps[:], func=ACT.Exp, scale=-1.0, bias=ln_half[:]
                 )
-            nc.scalar.copy(out=decayed[half][:, i, channels(c)], in_=decayed_ps[:])
+            for pair in range(PAIRS):
+                decayed_ps = banks.tile([P, 2, COLS], F32, tag="turned")
+                for r, j, part in parts(decayed_ps, c, pair):
+                    add_transposed(part, spread(vec_cols, j), True, False)
+                    nc.tensor.matmul(
+                        out=part, lhsT=identity_bf16[:], rhs=pp_sb[:, r, j * P : (j + 1) * P], start=False, stop=True
+                    )
+                nc.scalar.copy(out=decayed[:, pair_rows(pair), :], in_=decayed_ps[:])
+            return half_rho, decayed
 
-        def log_rows(r, j):
-            return log_bb[:, j, r * P : (r + 1) * P]
-
-        def reciprocal_of_bb(half, i, c):
-            log_ps = turned.tile([P, N_TILE], F32, tag="turned")
-            for j in range(BLOCKS_OF_TILE):
-                nc.tensor.transpose(
-                    log_ps[:, j * P : (j + 1) * P], log_rows(half * HALF_TILES + i, c * BLOCKS_OF_TILE + j), identity[:]
-                )
-            nc.scalar.activation(
-                out=half_rho[half][:, i, channels(c)], in_=log_ps[:], func=ACT.Exp, scale=-1.0, bias=ln_half[:]
-            )
-
-        def shifted_log(r, c):
-            shift_ps = shifts.tile([P, N_TILE], F32, tag="shift")
-            for j in range(BLOCKS_OF_TILE):
-                block = slice(j * P, (j + 1) * P)
-                add_transposed(shift_ps[:, block], log_rows(r, c * BLOCKS_OF_TILE + j), True, False)
-                add_transposed(shift_ps[:, block], spread(minus_both, c * BLOCKS_OF_TILE + j), False, True)
+        def shifted_log(c, pair):
+            shift_ps = banks.tile([P, 2, COLS], F32, tag="shift")
+            for r, j, part in parts(shift_ps, c, pair):
+                add_transposed(part, log_rows(r, j), True, False)
+                add_transposed(part, spread(minus_both, j), False, True)
             return shift_ps
 
-        def old_average(half, c):
-            for i in range(HALF_TILES):
-                nc.gpsimd.tensor_tensor(
-                    out=half_rho[half][:, i, channels(c)], in0=aa_sb[half][:, i, channels(c)],
-                    in1=half_rho[half][:, i, channels(c)], op=ALU.mult,
-                )
-
-        def regroup(engine_copy, mixed, grouped, g):
-            engine_copy(
-                out=grouped[:, g].rearrange("p (c i) t -> p c t i", i=4),
-                in_=mixed[:, g].rearrange("p t (c i) -> p c t i", i=4),
-            )
-
-        def mix_and_quantise(half, regroup_xk, regroup_xv):
-            xk_mixed = front.tile([P, PASSES, 4, HALF_ROWS], BF16, tag="xk_mixed")
-            xv_mixed = front.tile([P, PASSES, 4, HALF_ROWS], BF16, tag="xv_mixed")
-            xk_grouped = front.tile([P, PASSES, HALF_ROWS, 4], BF16, tag="xk_grouped", align_bytes=64)
-            xv_grouped = front.tile([P, PASSES, HALF_ROWS, 4], BF16, tag="xv_grouped", align_bytes=64)
+        def turn_weights(w_sb, tag, copy):
+            grouped = flow.tile([P, PASSES, 4 * COLS], BF16, tag=tag + "_grouped", bufs=1, align_bytes=64)
             for g in range(PASSES):
-                x_turned = turned.tile([P, 2, HALF_ROWS], F32, tag="turned")
-                alpha_turned = turned.tile([P, 2, HALF_ROWS], F32, tag="turned")
-                for act_turned, act_sb in ((x_turned, x_sb), (alpha_turned, alpha_sb)):
-                    for u in range(2):
-                        for i in range(HALF_TILES):
-                            block = act_sb[half][:, i, :].bitcast(F32)
-                            nc.tensor.transpose(
-                                act_turned[:, u, i * P : (i + 1) * P], block[:, every_second_word(g, u)], identity[:]
-                            )
+                w_turned = banks.tile([P, 2, COLS], F32, tag="turned")
                 for u in range(2):
-                    x_pairs = x_turned[:, u, :].bitcast(BF16).rearrange("p (b e) -> p b e", e=2)
-                    alpha_pairs = alpha_turned[:, u, :].bitcast(BF16).rearrange("p (b e) -> p b e", e=2)
-                    for e in range(2):
-                        for first_row, mixed in ((0, xk_mixed), (2, xv_mixed)):
-                            col = 2 * (first_row + g) + e
-                            alpha_part = front.tile([P, HALF_ROWS], F32, tag="alpha_part", bufs=6)
-                            nc.scalar.activation(
-                                out=alpha_part[:], in_=alpha_pairs[:, :, e], func=ACT.Copy,
-                                scale=one_minus_mix[:, u, col : col + 1],
-                            )
-                            nc.vector.scalar_tensor_tensor(
-                                out=mixed[:, g, 2 * u + e, :], in0=x_pairs[:, :, e], scalar=mix[:, u, col : col + 1],
-                                in1=alpha_part[:], op0=ALU.mult, op1=ALU.add,
-                            )
-                regroup(regroup_xk, xk_mixed, xk_grouped, g)
-                regroup(regroup_xv, xv_mixed, xv_grouped, g)
-            rows = slice(half * HALF_ROWS, (half + 1) * HALF_ROWS)
-            for g in range(PASSES):
-                for grouped, words, scales in ((xk_grouped, xk_words, xk_scales), (xv_grouped, xv_words, xv_scales)):
-                    nc.vector.quantize_mx(
-                        out=words[:, g, rows].bitcast(FP8X4), scales=scales[:, g, rows],
-                        in_=grouped[:, g].rearrange("p b t -> p (b t)"),
-                    )
-
-        def project(c, r, x_words, x_scales, w_words, w_scales, tag):
-            acc = sums.tile([P, N_TILE], F32, tag=tag)
-            rows = slice(r * P, (r + 1) * P)
-            for g in range(PASSES):
-                nc.tensor.matmul_mx(
-                    out=acc[:],
-                    lhsT=x_words[:, g, rows].bitcast(FP8X4), lhsT_scale=x_scales[:, g, rows],
-                    rhs=w_words[:, c, g, :].bitcast(FP8X4), rhs_scale=w_scales[:, c, g, :],
-                    start=(g == 0), stop=(g == PASSES - 1),
+                    for i in range(TILES_OF_BLOCK):
+                        nc.tensor.transpose(
+                            w_turned[:, u, i * P : (i + 1) * P],
+                            w_sb[:, i, :].bitcast(F32)[:, every_second_word(g, u)], identity[:],
+                        )
+                copy(
+                    out=grouped[:, g, :].bitcast(F32).rearrange("p (a u) -> p a u", u=2),
+                    in_=w_turned[:].rearrange("p u a -> p a u"),
                 )
+            return grouped
+
+        def quantise_weights(grouped, tag):
+            words = flow.tile([P, PASSES, COLS], U32, tag=tag + "_words", align_bytes=64)
+            scales = flow.tile([P, PASSES, COLS], U8, tag=tag + "_scales", align_bytes=64)
+            nc.vector.quantize_mx(
+                out=words[:].rearrange("p g a -> p (g a)").bitcast(FP8X4),
+                scales=scales[:].rearrange("p g a -> p (g a)"),
+                in_=grouped[:].rearrange("p g a -> p (g a)"),
+            )
+            return words, scales
+
+        def project(x_words, x_scales, w_words, w_scales, pair, tag):
+            acc = banks.tile([P, 2, COLS], F32, tag=tag)
+            for i in range(2):
+                rows = slice((2 * pair + i) * P, (2 * pair + i + 1) * P)
+                for g in range(PASSES):
+                    nc.tensor.matmul_mx(
+                        out=acc[:, i, :],
+                        lhsT=x_words[:, g, rows].bitcast(FP8X4), lhsT_scale=x_scales[:, g, rows],
+                        rhs=w_words[:, g, :].bitcast(FP8X4), rhs_scale=w_scales[:, g, :],
+                        start=(g == 0), stop=(g == PASSES - 1),
+                    )
             return acc
 
-        def output_pair(half, c, helper):
-            cols = channels(c)
-            tiles = range(HALF_TILES)
+        def block_tile(tag):
+            block = late.tile([P, ROW_TILES, COLS], F32, tag=tag)
+            return block
+
+        def store(out, c, block, pair=None):
+            tiles = slice(0, ROW_TILES) if pair is None else pair_rows(pair)
+            nc.sync.dma_start(out=rows_on_partitions(out)[:, tiles, channels(c)], in_=block[:, tiles, :])
+
+        def old_average(c, half_rho):
+            nc.vector.tensor_tensor(out=half_rho[:], in0=aa_sb[:, :, channels(c)], in1=half_rho[:], op=ALU.mult)
+
+        pairs = range(PAIRS)
+        wv_grouped = turn_weights(wv_sb[0], "wv", nc.scalar.copy)
+        wk_grouped = turn_weights(wk_sb[0], "wk", nc.vector.tensor_copy)
+        for j in range(CH_TILES):
+            bb_turned = banks.tile([P, B], BF16, tag="shift")
+            for r in range(ROW_TILES):
+                nc.tensor.transpose(
+                    bb_turned[:, r * P : (r + 1) * P], bb_sb[:, r, j * P : (j + 1) * P], identity_bf16[:]
+                )
+            nc.scalar.activation(out=log_bb[:, j, :], in_=bb_turned[:], func=ACT.Ln, bias=tiny[:])
+
+        half_rho, decayed = prepare_state(0)
+        wk = quantise_weights(wk_grouped, "wk")
+        wv = quantise_weights(wv_grouped, "wv")
+        old_average(0, half_rho)
+        for c in range(COL_BLOCKS):
+            last = c == COL_BLOCKS - 1
             k_ps = []
             v_ps = []
-            for i in tiles:
-                k_ps.append(project(c, half * HALF_TILES + i, xk_words, xk_scales, wk_words, wk_scales, "k"))
-            for i in tiles:
-                v_ps.append(project(c, half * HALF_TILES + i, xv_words, xv_scales, wv_words, wv_scales, "v"))
-            decayed_tiles = decayed[half][:, :, cols]
+            shift_ps = []
+            for pair in pairs:
+                k_ps.append(project(xk_words, xk_scales, wk[0], wk[1], pair, "k"))
+            for pair in pairs:
+                v_ps.append(project(xv_words, xv_scales, wv[0], wv[1], pair, "v"))
+            if not last:
+                wk_grouped = turn_weights(wk_sb[c + 1], "wk", nc.scalar.copy)
+                wv_grouped = turn_weights(wv_sb[c + 1], "wv", nc.scalar.copy)
+            for pair in pairs:
+                shift_ps.append(shifted_log(c, pair))
 
-            def pair_tile(tag):
-                pair = late.tile([P, HALF_TILES, N_TILE], F32, tag=tag)
-                return pair
-
-            d2 = pair_tile("d2")
-            gate = pair_tile("gate")
-            qq2 = pair_tile("qq2")
-            for i in tiles:
-                nc.vector.tensor_tensor(out=d2[:, i, :], in0=k_ps[i][:], in1=decayed_tiles[:, i, :], op=ALU.subtract)
-            for i in tiles:
-                shift_ps = shifted_log(half * HALF_TILES + i, c)
-                nc.vector.tensor_tensor(out=gate[:, i, :], in0=d2[:, i, :], in1=shift_ps[:], op=ALU.subtract)
-                nc.vector.tensor_tensor(out=qq2[:, i, :], in0=k_ps[i][:], in1=decayed_tiles[:, i, :], op=ALU.max)
-            nc.sync.dma_start(out=half_rows(out_3, half)[:, :, cols], in_=qq2[:])
-            swing = pair_tile("swing")
-            wkv = pair_tile("wkv")
-            for i in tiles:
+            d2 = block_tile("d2")
+            gate = block_tile("gate")
+            qq2 = block_tile("qq2")
+            swing = block_tile("swing")
+            wkv = block_tile("wkv")
+            for pair in pairs:
+                tiles = pair_rows(pair)
+                nc.vector.tensor_tensor(
+                    out=d2[:, tiles, :], in0=k_ps[pair][:], in1=decayed[:, tiles, :], op=ALU.subtract
+                )
+            for pair in pairs:
+                tiles = pair_rows(pair)
+                nc.vector.tensor_tensor(
+                    out=gate[:, tiles, :], in0=d2[:, tiles, :], in1=shift_ps[pair][:], op=ALU.subtract
+                )
+            for pair in pairs:
+                tiles = pair_rows(pair)
+                nc.vector.tensor_tensor(
+                    out=qq2[:, tiles, :], in0=k_ps[pair][:], in1=decayed[:, tiles, :], op=ALU.max
+                )
+            store(out_3, c, qq2)
+            for pair in pairs:
+                tiles = pair_rows(pair)
                 nc.vector.scalar_tensor_tensor(
-                    out=swing[:, i, :], in0=v_ps[i][:], scalar=0.5, in1=half_rho[half][:, i, cols],
+                    out=swing[:, tiles, :], in0=v_ps[pair][:], scalar=0.5, in1=half_rho[:, tiles, :],
                     op0=ALU.mult, op1=ALU.subtract,
                 )
-            for i in tiles:
+            for pair in pairs:
+                tiles = pair_rows(pair)
                 nc.vector.scalar_tensor_tensor(
-                    out=wkv[:, i, :], in0=v_ps[i][:], scalar=0.5, in1=half_rho[half][:, i, cols],
+                    out=wkv[:, tiles, :], in0=v_ps[pair][:], scalar=0.5, in1=half_rho[:, tiles, :],
                     op0=ALU.mult, op1=ALU.add,
                 )
 
-            grow_old = pair_tile("grow_old")
+            grow_old = block_tile("grow_old")
             nc.scalar.activation(out=grow_old[:], in_=d2[:], func=ACT.Exp, scale=-1.0)
             grow_new = d2
             nc.scalar.activation(out=grow_new[:], in_=d2[:], func=ACT.Exp)
             nc.scalar.activation(out=gate[:], in_=gate[:], func=ACT.Tanh, scale=0.5)
 
-            new_part = pair_tile("new_part")
-            for i in tiles:
+            if not last:
+                half_rho, decayed = prepare_state(c + 1)
+
+            next_bb = block_tile("next_bb")
+            nc.vector.scalar_tensor_tensor(
+                out=next_bb[:], in0=grow_old[:], scalar=1.0, in1=bb_sb[:, :, channels(c)],
+                op0=ALU.min, op1=ALU.mult,
+            )
+            new_part = block_tile("new_part")
+            for pair in pairs:
+                tiles = pair_rows(pair)
                 nc.vector.scalar_tensor_tensor(
-                    out=new_part[:, i, :], in0=grow_new[:, i, :], scalar=1.0, in1=v_ps[i][:], op0=ALU.min, op1=ALU.mult
+                    out=new_part[:, tiles, :], in0=grow_new[:, tiles, :], scalar=1.0, in1=v_ps[pair][:],
+                    op0=ALU.min, op1=ALU.mult,
                 )
-            next_aa = pair_tile("next_aa")
-            nc.vector.scalar_tensor_tensor(
-                out=next_aa[:], in0=grow_old[:], scalar=1.0, in1=aa_sb[half][:, :, cols], op0=ALU.min, op1=ALU.mult
-            )
-            next_bb = grow_old
-            nc.vector.scalar_tensor_tensor(
-                out=next_bb[:], in0=grow_old[:], scalar=1.0, in1=bb_sb[half][:, :, cols], op0=ALU.min, op1=ALU.mult
-            )
             nc.vector.scalar_tensor_tensor(
                 out=next_bb[:], in0=grow_new[:], scalar=1.0, in1=next_bb[:], op0=ALU.min, op1=ALU.add
             )
-            nc.sync.dma_start(out=half_rows(out_2, half)[:, :, cols], in_=next_bb[:])
-            for i in tiles:
-                helper.tensor_tensor(out=swing[:, i, :], in0=gate[:, i, :], in1=swing[:, i, :], op=ALU.mult)
-            for i in tiles:
-                helper.tensor_tensor(out=wkv[:, i, :], in0=wkv[:, i, :], in1=swing[:, i, :], op=ALU.add)
-            nc.sync.dma_start(out=half_rows(out_0, half)[:, :, cols], in_=wkv[:])
-            for i in tiles:
-                helper.tensor_tensor(out=next_aa[:, i, :], in0=next_aa[:, i, :], in1=new_part[:, i, :], op=ALU.add)
-            nc.sync.dma_start(out=half_rows(out_1, half)[:, :, cols], in_=next_aa[:])
-
-        def prepare_state(half, c):
-            for i in range(HALF_TILES):
-                decay_pp(half, i, c)
-            for i in range(HALF_TILES):
-                reciprocal_of_bb(half, i, c)
-            old_average(half, c)
-
-        both = (nc.scalar.copy, nc.vector.tensor_copy)
-        scalar_alone = (nc.scalar.copy, nc.scalar.copy)
-        mix_and_quantise(0, nc.vector.tensor_copy, nc.scalar.copy)
-        for j in range(CH_BLOCKS):
-            logarithm_of_bb(j)
-        prepare_state(0, 0)
-        quantise_weight_half(wk_sb[0], wk_words, wk_scales, 0, both)
-        quantise_weight_half(wv_sb[0], wv_words, wv_scales, 0, both)
-        output_pair(0, 0, nc.vector)
-        quantise_weight_half(wk_sb[1], wk_words, wk_scales, 1, scalar_alone)
-        quantise_weight_half(wv_sb[1], wv_words, wv_scales, 1, scalar_alone)
-        prepare_state(0, 1)
-        mix_and_quantise(1, nc.scalar.copy, nc.scalar.copy)
-        prepare_state(1, 0)
-        output_pair(0, 1, nc.vector)
-        prepare_state(1, 1)
-        output_pair(1, 0, nc.vector)
-        output_pair(1, 1, nc.vector)
+            store(out_2, c, next_bb)
+            if not last:
+                old_average(c + 1, half_rho)
+                wk = quantise_weights(wk_grouped, "wk")
+                wv = quantise_weights(wv_grouped, "wv")
+            next_aa = grow_old
+            nc.vector.scalar_tensor_tensor(
+                out=next_aa[:], in0=grow_old[:], scalar=1.0, in1=aa_sb[:, :, channels(c)],
+                op0=ALU.min, op1=ALU.mult,
+            )
+            helper = nc.vector if last else nc.gpsimd
+            for pair in pairs:
+                tiles = pair_rows(pair)
+                helper.tensor_tensor(
+                    out=next_aa[:, tiles, :], in0=next_aa[:, tiles, :], in1=new_part[:, tiles, :], op=ALU.add
+                )
+                store(out_1, c, next_aa, pair)
+            for pair in pairs:
+                tiles = pair_rows(pair)
+                helper.tensor_tensor(
+                    out=swing[:, tiles, :], in0=gate[:, tiles, :], in1=swing[:, tiles, :], op=ALU.mult
+                )
+            for pair in pairs:
+                tiles = pair_rows(pair)
+                helper.tensor_tensor(
+                    out=wkv[:, tiles, :], in0=wkv[:, tiles, :], in1=swing[:, tiles, :], op=ALU.add
+                )
+                store(out_0, c, wkv, pair)

@@ -15,15 +15,13 @@ ACT = mybir.ActivationFunctionType
 B, H, A = 512, 1024, 1024
 P = 128
 ROW_TILES = B // P
-PAIRS = ROW_TILES // 2
 K_PASS = 4 * P
 PASSES = H // K_PASS
 PASS_WORDS = K_PASS // 2
-COLS = 256
-COL_BLOCKS = A // COLS
 CH_TILES = A // P
-TILES_OF_BLOCK = COLS // P
-LN_HALF = math.log(0.5)
+LOAD_TILES = 2
+HALF_COLS = A // 2
+LN_2 = math.log(2.0)
 TINY = 2.0 ** -60
 
 FLOPS = 2 * 2 * B * H * A
@@ -48,8 +46,8 @@ def tile_rwkvtimemix_pa_kernel(
         def every_second_word(g, u):
             return slice(g * PASS_WORDS + u, (g + 1) * PASS_WORDS, 2)
 
-        def channels(c):
-            return slice(c * COLS, (c + 1) * COLS)
+        def tile_channels(t):
+            return slice(t * P, (t + 1) * P)
 
         mix_rows = const.tile([P, K_PASS], BF16)
         nc.gpsimd.memset(mix_rows[:], 0.0)
@@ -66,31 +64,36 @@ def tile_rwkvtimemix_pa_kernel(
             nc.sync.dma_start(out=x_sb[:, :, h_cols], in_=rows_on_partitions(x)[:, :, h_cols])
             nc.sync.dma_start(out=alpha_sb[:, :, h_cols], in_=rows_on_partitions(alpha)[:, :, h_cols])
 
-        def load_state(state, name):
-            state_sb = keep.tile([P, ROW_TILES, A], BF16, name=name)
-            nc.sync.dma_start(out=state_sb[:], in_=rows_on_partitions(state))
-            return state_sb
+        aa_sb = keep.tile([P, ROW_TILES, A], BF16)
+        bb_sb = keep.tile([P, ROW_TILES, A], BF16)
+        pp_sb = keep.tile([P, ROW_TILES, A], BF16)
 
-        def load_weights(w, c, tag):
-            w_sb = flow.tile([P, TILES_OF_BLOCK, H], BF16, tag=tag)
-            nc.sync.dma_start(out=w_sb[:], in_=w[channels(c), :].rearrange("(i p) n -> p i n", p=P))
-            return w_sb
+        def load_state_half(half):
+            cols = slice(half * HALF_COLS, (half + 1) * HALF_COLS)
+            for state_sb, state in ((bb_sb, bb), (pp_sb, pp), (aa_sb, aa)):
+                nc.sync.dma_start(out=state_sb[:, :, cols], in_=rows_on_partitions(state)[:, :, cols])
 
-        bb_sb = load_state(bb, "bb_sb")
-        wk_sb = [load_weights(Wk, 0, "wk")]
-        wv_sb = [load_weights(Wv, 0, "wv")]
-        pp_sb = load_state(pp, "pp_sb")
-        aa_sb = load_state(aa, "aa_sb")
-        for c in range(1, COL_BLOCKS):
-            wk_sb.append(load_weights(Wk, c, "wk"))
-            wv_sb.append(load_weights(Wv, c, "wv"))
+        def load_weights(n):
+            channels = slice(n * LOAD_TILES * P, (n + 1) * LOAD_TILES * P)
+            loaded = []
+            for w, tag in ((Wk, "wk"), (Wv, "wv")):
+                w_sb = flow.tile([P, LOAD_TILES, H], BF16, tag=tag)
+                nc.sync.dma_start(out=w_sb[:], in_=w[channels, :].rearrange("(i p) n -> p i n", p=P))
+                loaded.append(w_sb)
+            return loaded
+
+        w_sb = [load_weights(0)]
+        load_state_half(0)
+        load_state_half(1)
+        for n in range(1, CH_TILES // LOAD_TILES):
+            w_sb.append(load_weights(n))
 
         tiny = const.tile([P, 1], F32)
         nc.vector.memset(tiny[:], TINY)
         warm = const.tile([P, 1], F32)
         nc.scalar.activation(out=warm[:], in_=tiny[:], func=ACT.Ln)
-        ln_half = const.tile([P, 1], F32)
-        nc.vector.tensor_scalar(out=ln_half[:], in0=tiny[:], scalar1=0.0, scalar2=LN_HALF, op0=ALU.mult, op1=ALU.add)
+        ln_2 = const.tile([P, 1], F32)
+        nc.vector.tensor_scalar(out=ln_2[:], in0=tiny[:], scalar1=0.0, scalar2=LN_2, op0=ALU.mult, op1=ALU.add)
         identity = const.tile([P, P], F32)
         make_identity(nc, identity[:])
         identity_bf16 = const.tile([P, P], BF16)
@@ -98,9 +101,9 @@ def tile_rwkvtimemix_pa_kernel(
         mix = const.tile([P, 2, 8], F32)
         one_minus_mix = const.tile([P, 2, 8], F32)
         vec_cols = const.tile([P, 2 * CH_TILES], F32)
-        minus_both = const.tile([P, CH_TILES], F32)
+        half_both = const.tile([P, CH_TILES], F32)
 
-        order_kept = {mybir.EngineType.DVE, mybir.EngineType.Pool, mybir.EngineType.Activation}
+        order_kept = {mybir.EngineType.DVE, mybir.EngineType.Activation, mybir.EngineType.PE}
         stack.enter_context(tc.manual_schedule(engines=order_kept))
 
         mix_turned = banks.tile([P, 2, P], F32, tag="turned")
@@ -114,10 +117,10 @@ def tile_rwkvtimemix_pa_kernel(
         vec_turned = banks.tile([P, P], BF16, tag="turned")
         nc.tensor.transpose(vec_turned[:], vec_rows[:], identity_bf16[:])
         nc.vector.tensor_copy(out=vec_cols[:], in_=vec_turned[:, 0 : 2 * CH_TILES])
-        nc.vector.scalar_tensor_tensor(
-            out=minus_both[:], in0=vec_cols[:, 0:CH_TILES], scalar=-1.0, in1=vec_cols[:, CH_TILES : 2 * CH_TILES],
-            op0=ALU.mult, op1=ALU.subtract,
+        nc.vector.tensor_tensor(
+            out=half_both[:], in0=vec_cols[:, 0:CH_TILES], in1=vec_cols[:, CH_TILES : 2 * CH_TILES], op=ALU.add
         )
+        nc.vector.tensor_scalar(out=half_both[:], in0=half_both[:], scalar1=0.5, scalar2=None, op0=ALU.mult)
 
         xk_words = keep.tile([P, PASSES, B], U32, align_bytes=64)
         xk_scales = keep.tile([P, PASSES, B], U8, align_bytes=64)
@@ -136,8 +139,8 @@ def tile_rwkvtimemix_pa_kernel(
         xv_grouped = front.tile([P, PASSES, B, 4], BF16, align_bytes=64)
         for g in range(PASSES):
             for u in range(2):
-                x_turned = banks.tile([P, B], F32, tag="k")
-                alpha_turned = banks.tile([P, B], F32, tag="v")
+                x_turned = banks.tile([P, B], F32, tag="out")
+                alpha_turned = banks.tile([P, B], F32, tag="state")
                 for act_turned, act_sb in ((alpha_turned, alpha_sb), (x_turned, x_sb)):
                     for r in range(ROW_TILES):
                         nc.tensor.transpose(
@@ -167,73 +170,23 @@ def tile_rwkvtimemix_pa_kernel(
                     in_=grouped[:, g].rearrange("p b t -> p (b t)"),
                 )
 
-        log_bb = keep.tile([P, CH_TILES, B], F32)
-
-        def log_rows(r, j):
-            return log_bb[:, j, r * P : (r + 1) * P]
-
-        def spread(columns, j):
-            return columns[:, j : j + 1].to_broadcast([P, P])
-
-        def add_transposed(out, block, start, stop):
-            nc.tensor.matmul(out=out, lhsT=block, rhs=identity[:], start=start, stop=stop, is_transpose=True)
-
-        def parts(bank, c, pair):
-            return [
-                (2 * pair + i, c * TILES_OF_BLOCK + j, bank[:, i, j * P : (j + 1) * P])
-                for i in range(2)
-                for j in range(TILES_OF_BLOCK)
-            ]
-
-        def pair_rows(pair):
-            return slice(2 * pair, 2 * pair + 2)
-
-        def prepare_state(c):
-            half_rho = flow.tile([P, ROW_TILES, COLS], F32, tag="half_rho")
-            decayed = flow.tile([P, ROW_TILES, COLS], F32, tag="decayed")
-            for pair in range(PAIRS):
-                log_ps = banks.tile([P, 2, COLS], F32, tag="turned")
-                for r, j, part in parts(log_ps, c, pair):
-                    nc.tensor.transpose(part, log_rows(r, j), identity[:])
-                nc.scalar.activation(
-                    out=half_rho[:, pair_rows(pair), :], in_=log_ps[:], func=ACT.Exp, scale=-1.0, bias=ln_half[:]
-                )
-            for pair in range(PAIRS):
-                decayed_ps = banks.tile([P, 2, COLS], F32, tag="turned")
-                for r, j, part in parts(decayed_ps, c, pair):
-                    add_transposed(part, spread(vec_cols, j), True, False)
-                    nc.tensor.matmul(
-                        out=part, lhsT=identity_bf16[:], rhs=pp_sb[:, r, j * P : (j + 1) * P], start=False, stop=True
-                    )
-                nc.scalar.copy(out=decayed[:, pair_rows(pair), :], in_=decayed_ps[:])
-            return half_rho, decayed
-
-        def shifted_log(c, pair):
-            shift_ps = banks.tile([P, 2, COLS], F32, tag="shift")
-            for r, j, part in parts(shift_ps, c, pair):
-                add_transposed(part, log_rows(r, j), True, False)
-                add_transposed(part, spread(minus_both, j), False, True)
-            return shift_ps
-
-        def turn_weights(w_sb, tag, copy):
-            grouped = flow.tile([P, PASSES, 4 * COLS], BF16, tag=tag + "_grouped", bufs=1, align_bytes=64)
+        def turn_weights(t, which, copy):
+            tag = ("wk", "wv")[which]
+            words = w_sb[t // LOAD_TILES][which][:, t % LOAD_TILES, :].bitcast(F32)
+            grouped = flow.tile([P, PASSES, 4 * P], BF16, tag=tag + "_grouped", align_bytes=64)
+            w_turned = banks.tile([P, PASSES, 2, P], F32, tag="turned")
             for g in range(PASSES):
-                w_turned = banks.tile([P, 2, COLS], F32, tag="turned")
                 for u in range(2):
-                    for i in range(TILES_OF_BLOCK):
-                        nc.tensor.transpose(
-                            w_turned[:, u, i * P : (i + 1) * P],
-                            w_sb[:, i, :].bitcast(F32)[:, every_second_word(g, u)], identity[:],
-                        )
-                copy(
-                    out=grouped[:, g, :].bitcast(F32).rearrange("p (a u) -> p a u", u=2),
-                    in_=w_turned[:].rearrange("p u a -> p a u"),
-                )
+                    nc.tensor.transpose(w_turned[:, g, u, :], words[:, every_second_word(g, u)], identity[:])
+            copy(
+                out=grouped[:].bitcast(F32).rearrange("p g (a u) -> p g a u", u=2),
+                in_=w_turned[:].rearrange("p g u a -> p g a u"),
+            )
             return grouped
 
         def quantise_weights(grouped, tag):
-            words = flow.tile([P, PASSES, COLS], U32, tag=tag + "_words", align_bytes=64)
-            scales = flow.tile([P, PASSES, COLS], U8, tag=tag + "_scales", align_bytes=64)
+            words = flow.tile([P, PASSES, P], U32, tag=tag + "_words", align_bytes=64)
+            scales = flow.tile([P, PASSES, P], U8, tag=tag + "_scales", align_bytes=64)
             nc.vector.quantize_mx(
                 out=words[:].rearrange("p g a -> p (g a)").bitcast(FP8X4),
                 scales=scales[:].rearrange("p g a -> p (g a)"),
@@ -241,143 +194,165 @@ def tile_rwkvtimemix_pa_kernel(
             )
             return words, scales
 
-        def project(x_words, x_scales, w_words, w_scales, pair, tag):
-            acc = banks.tile([P, 2, COLS], F32, tag=tag)
-            for i in range(2):
-                rows = slice((2 * pair + i) * P, (2 * pair + i + 1) * P)
-                for g in range(PASSES):
-                    nc.tensor.matmul_mx(
-                        out=acc[:, i, :],
-                        lhsT=x_words[:, g, rows].bitcast(FP8X4), lhsT_scale=x_scales[:, g, rows],
-                        rhs=w_words[:, g, :].bitcast(FP8X4), rhs_scale=w_scales[:, g, :],
-                        start=(g == 0), stop=(g == PASSES - 1),
-                    )
+        def project(weights, x_words, x_scales, tag):
+            words, scales = weights
+            acc = banks.tile([P, B], F32, tag=tag, bufs=1)
+            for g in range(PASSES):
+                nc.tensor.matmul_mx(
+                    out=acc[:],
+                    lhsT=words[:, g, :].bitcast(FP8X4), lhsT_scale=scales[:, g, :],
+                    rhs=x_words[:, g, :].bitcast(FP8X4), rhs_scale=x_scales[:, g, :],
+                    start=(g == 0), stop=(g == PASSES - 1),
+                )
             return acc
 
-        def block_tile(tag):
-            block = late.tile([P, ROW_TILES, COLS], F32, tag=tag)
-            return block
-
-        def store(out, c, block, pair=None):
-            tiles = slice(0, ROW_TILES) if pair is None else pair_rows(pair)
-            nc.sync.dma_start(out=rows_on_partitions(out)[:, tiles, channels(c)], in_=block[:, tiles, :])
-
-        def old_average(c, half_rho):
-            nc.vector.tensor_tensor(out=half_rho[:], in0=aa_sb[:, :, channels(c)], in1=half_rho[:], op=ALU.mult)
-
-        pairs = range(PAIRS)
-        wv_grouped = turn_weights(wv_sb[0], "wv", nc.scalar.copy)
-        wk_grouped = turn_weights(wk_sb[0], "wk", nc.vector.tensor_copy)
-        for j in range(CH_TILES):
-            bb_turned = banks.tile([P, B], BF16, tag="shift")
+        def turn_state(out, state_sb, t):
             for r in range(ROW_TILES):
                 nc.tensor.transpose(
-                    bb_turned[:, r * P : (r + 1) * P], bb_sb[:, r, j * P : (j + 1) * P], identity_bf16[:]
-                )
-            nc.scalar.activation(out=log_bb[:, j, :], in_=bb_turned[:], func=ACT.Ln, bias=tiny[:])
-
-        half_rho, decayed = prepare_state(0)
-        wk = quantise_weights(wk_grouped, "wk")
-        wv = quantise_weights(wv_grouped, "wv")
-        old_average(0, half_rho)
-        for c in range(COL_BLOCKS):
-            last = c == COL_BLOCKS - 1
-            k_ps = []
-            v_ps = []
-            shift_ps = []
-            for pair in pairs:
-                k_ps.append(project(xk_words, xk_scales, wk[0], wk[1], pair, "k"))
-            for pair in pairs:
-                v_ps.append(project(xv_words, xv_scales, wv[0], wv[1], pair, "v"))
-            if not last:
-                wk_grouped = turn_weights(wk_sb[c + 1], "wk", nc.scalar.copy)
-                wv_grouped = turn_weights(wv_sb[c + 1], "wv", nc.scalar.copy)
-            for pair in pairs:
-                shift_ps.append(shifted_log(c, pair))
-
-            d2 = block_tile("d2")
-            gate = block_tile("gate")
-            qq2 = block_tile("qq2")
-            swing = block_tile("swing")
-            wkv = block_tile("wkv")
-            for pair in pairs:
-                tiles = pair_rows(pair)
-                nc.vector.tensor_tensor(
-                    out=d2[:, tiles, :], in0=k_ps[pair][:], in1=decayed[:, tiles, :], op=ALU.subtract
-                )
-            for pair in pairs:
-                tiles = pair_rows(pair)
-                nc.vector.tensor_tensor(
-                    out=gate[:, tiles, :], in0=d2[:, tiles, :], in1=shift_ps[pair][:], op=ALU.subtract
-                )
-            for pair in pairs:
-                tiles = pair_rows(pair)
-                nc.vector.tensor_tensor(
-                    out=qq2[:, tiles, :], in0=k_ps[pair][:], in1=decayed[:, tiles, :], op=ALU.max
-                )
-            store(out_3, c, qq2)
-            for pair in pairs:
-                tiles = pair_rows(pair)
-                nc.vector.scalar_tensor_tensor(
-                    out=swing[:, tiles, :], in0=v_ps[pair][:], scalar=0.5, in1=half_rho[:, tiles, :],
-                    op0=ALU.mult, op1=ALU.subtract,
-                )
-            for pair in pairs:
-                tiles = pair_rows(pair)
-                nc.vector.scalar_tensor_tensor(
-                    out=wkv[:, tiles, :], in0=v_ps[pair][:], scalar=0.5, in1=half_rho[:, tiles, :],
-                    op0=ALU.mult, op1=ALU.add,
+                    out[:, r * P : (r + 1) * P], state_sb[:, r, tile_channels(t)], identity_bf16[:]
                 )
 
-            grow_old = block_tile("grow_old")
-            nc.scalar.activation(out=grow_old[:], in_=d2[:], func=ACT.Exp, scale=-1.0)
-            grow_new = d2
+        def turn_aa_bb(t):
+            turned = banks.tile([P, 2, B], BF16, tag="state")
+            turn_state(turned[:, 0, :], aa_sb, t)
+            turn_state(turned[:, 1, :], bb_sb, t)
+            return turned
+
+        def turn_pp(t):
+            turned = banks.tile([P, B], BF16, tag="turned")
+            turn_state(turned, pp_sb, t)
+            return turned
+
+        def copy_pp(turned):
+            pp_t = flow.tile([P, B], BF16, tag="pp_t")
+            nc.scalar.copy(out=pp_t[:], in_=turned[:])
+            return pp_t
+
+        def late_tile(tag):
+            tile = late.tile([P, B], F32, tag=tag)
+            return tile
+
+        log_bb = keep.tile([P, CH_TILES, B], F32)
+
+        def two_over_bb(t):
+            two_rho = late_tile("two_rho")
+            nc.scalar.activation(out=two_rho[:], in_=log_bb[:, t, :], func=ACT.Exp, scale=-1.0, bias=ln_2[:])
+            return two_rho
+
+        results = {}
+
+        def bring_back(t, out, sources, copy):
+            n, i = divmod(t, LOAD_TILES)
+            turned = banks.tile([P, ROW_TILES, P], F32, tag="out")
+            for r in range(ROW_TILES):
+                for s, source in enumerate(sources):
+                    nc.tensor.matmul(
+                        out=turned[:, r, :], lhsT=source[:, r * P : (r + 1) * P], rhs=identity[:],
+                        start=(s == 0), stop=(s == len(sources) - 1), is_transpose=True,
+                    )
+            if (out, n) not in results:
+                result = late.tile([P, ROW_TILES, LOAD_TILES * P], F32, tag="out_%d" % out)
+                results[(out, n)] = result
+            result = results[(out, n)]
+            cols = slice(i * P, (i + 1) * P)
+            copy(result[:, :, cols], turned[:])
+            dram = rows_on_partitions((out_0, out_1, out_2, out_3)[out])
+            if n == CH_TILES // LOAD_TILES - 1:
+                nc.sync.dma_start(out=dram[:, :, tile_channels(t)], in_=result[:, :, cols])
+            elif i == LOAD_TILES - 1:
+                nc.sync.dma_start(out=dram[:, :, n * LOAD_TILES * P : (n + 1) * LOAD_TILES * P], in_=result[:])
+
+        def scalar_copy(dst, src):
+            nc.scalar.copy(out=dst, in_=src)
+
+        def scalar_half(dst, src):
+            nc.scalar.activation(out=dst, in_=src, func=ACT.Copy, scale=0.5)
+
+        def vector_copy(dst, src):
+            nc.vector.tensor_copy(out=dst, in_=src)
+
+        grouped = [[turn_weights(0, 0, nc.scalar.copy), turn_weights(0, 1, nc.scalar.copy)]]
+        wk = quantise_weights(grouped[0][0], "wk")
+        wv = quantise_weights(grouped[0][1], "wv")
+        for t in range(CH_TILES):
+            bb_turned = banks.tile([P, B], BF16, tag="out")
+            turn_state(bb_turned, bb_sb, t)
+            nc.scalar.activation(out=log_bb[:, t, :], in_=bb_turned[:], func=ACT.Ln, bias=tiny[:])
+        state = turn_aa_bb(0)
+        pp_t = copy_pp(turn_pp(0))
+        two_rho = two_over_bb(0)
+        grouped.append([turn_weights(1, 0, nc.scalar.copy), turn_weights(1, 1, nc.scalar.copy)])
+        k_ps = project(wk, xk_words, xk_scales, "k")
+        v_ps = project(wv, xv_words, xv_scales, "v")
+
+        done = None
+        for t in range(CH_TILES):
+            more = t + 1 < CH_TILES
+            decay = vec_cols[:, t : t + 1]
+            if more:
+                next_state = turn_aa_bb(t + 1)
+                next_pp = turn_pp(t + 1)
+
+            d2 = late_tile("d2")
+            nc.vector.scalar_tensor_tensor(
+                out=d2[:], in0=k_ps[:], scalar=decay, in1=pp_t[:], op0=ALU.subtract, op1=ALU.subtract
+            )
+            grow_new = late_tile("grow_new")
             nc.scalar.activation(out=grow_new[:], in_=d2[:], func=ACT.Exp)
-            nc.scalar.activation(out=gate[:], in_=gate[:], func=ACT.Tanh, scale=0.5)
+            nc.vector.tensor_tensor(out=two_rho[:], in0=state[:, 0, :], in1=two_rho[:], op=ALU.mult)
+            gate = late_tile("gate")
+            nc.vector.tensor_tensor(out=gate[:], in0=d2[:], in1=log_bb[:, t, :], op=ALU.subtract)
+            grow_old = late_tile("grow_old")
+            nc.scalar.activation(out=grow_old[:], in_=d2[:], func=ACT.Exp, scale=-1.0)
+            swing = late_tile("swing")
+            nc.vector.scalar_tensor_tensor(
+                out=swing[:], in0=two_rho[:], scalar=-0.5, in1=v_ps[:], op0=ALU.mult, op1=ALU.add
+            )
+            if more:
+                next_pp_t = copy_pp(next_pp)
+            nc.scalar.activation(
+                out=gate[:], in_=gate[:], func=ACT.Tanh, scale=0.5, bias=half_both[:, t : t + 1]
+            )
+            qq2 = late_tile("qq2")
+            nc.vector.scalar_tensor_tensor(
+                out=qq2[:], in0=pp_t[:], scalar=decay, in1=k_ps[:], op0=ALU.add, op1=ALU.max
+            )
+            if more:
+                wk = quantise_weights(grouped[t + 1][0], "wk")
+                wv = quantise_weights(grouped[t + 1][1], "wv")
 
-            if not last:
-                half_rho, decayed = prepare_state(c + 1)
+            if done is not None:
+                bring_back(t - 1, 3, done[3], scalar_copy)
+                bring_back(t - 1, 1, done[1], scalar_copy)
+            if t + 2 < CH_TILES:
+                grouped.append([turn_weights(t + 2, 0, nc.scalar.copy), turn_weights(t + 2, 1, nc.scalar.copy)])
+            if done is not None:
+                bring_back(t - 1, 2, done[2], scalar_copy)
+                bring_back(t - 1, 0, done[0], scalar_half)
+            if more:
+                next_two_rho = two_over_bb(t + 1)
 
-            next_bb = block_tile("next_bb")
+            e2b = late_tile("e2b")
+            nc.vector.tensor_scalar(out=e2b[:], in0=grow_new[:], scalar1=1.0, scalar2=None, op0=ALU.min)
+            old_aa = late_tile("old_aa")
             nc.vector.scalar_tensor_tensor(
-                out=next_bb[:], in0=grow_old[:], scalar=1.0, in1=bb_sb[:, :, channels(c)],
-                op0=ALU.min, op1=ALU.mult,
+                out=old_aa[:], in0=grow_old[:], scalar=1.0, in1=state[:, 0, :], op0=ALU.min, op1=ALU.mult
             )
-            new_part = block_tile("new_part")
-            for pair in pairs:
-                tiles = pair_rows(pair)
-                nc.vector.scalar_tensor_tensor(
-                    out=new_part[:, tiles, :], in0=grow_new[:, tiles, :], scalar=1.0, in1=v_ps[pair][:],
-                    op0=ALU.min, op1=ALU.mult,
-                )
+            new_aa = late_tile("new_aa")
+            nc.vector.tensor_tensor(out=new_aa[:], in0=e2b[:], in1=v_ps[:], op=ALU.mult)
+            old_bb = late_tile("old_bb")
             nc.vector.scalar_tensor_tensor(
-                out=next_bb[:], in0=grow_new[:], scalar=1.0, in1=next_bb[:], op0=ALU.min, op1=ALU.add
+                out=old_bb[:], in0=grow_old[:], scalar=1.0, in1=state[:, 1, :], op0=ALU.min, op1=ALU.mult
             )
-            store(out_2, c, next_bb)
-            if not last:
-                old_average(c + 1, half_rho)
-                wk = quantise_weights(wk_grouped, "wk")
-                wv = quantise_weights(wv_grouped, "wv")
-            next_aa = grow_old
             nc.vector.scalar_tensor_tensor(
-                out=next_aa[:], in0=grow_old[:], scalar=1.0, in1=aa_sb[:, :, channels(c)],
-                op0=ALU.min, op1=ALU.mult,
+                out=swing[:], in0=gate[:], scalar=1.0, in1=swing[:], op0=ALU.add, op1=ALU.mult
             )
-            helper = nc.vector if last else nc.gpsimd
-            for pair in pairs:
-                tiles = pair_rows(pair)
-                helper.tensor_tensor(
-                    out=next_aa[:, tiles, :], in0=next_aa[:, tiles, :], in1=new_part[:, tiles, :], op=ALU.add
-                )
-                store(out_1, c, next_aa, pair)
-            for pair in pairs:
-                tiles = pair_rows(pair)
-                helper.tensor_tensor(
-                    out=swing[:, tiles, :], in0=gate[:, tiles, :], in1=swing[:, tiles, :], op=ALU.mult
-                )
-            for pair in pairs:
-                tiles = pair_rows(pair)
-                helper.tensor_tensor(
-                    out=wkv[:, tiles, :], in0=wkv[:, tiles, :], in1=swing[:, tiles, :], op=ALU.add
-                )
-                store(out_0, c, wkv, pair)
+            done = ((two_rho, swing), (old_aa, new_aa), (old_bb, e2b), (qq2,))
+            if more:
+                k_ps = project(wk, xk_words, xk_scales, "k")
+                v_ps = project(wv, xv_words, xv_scales, "v")
+                state, pp_t, two_rho = next_state, next_pp_t, next_two_rho
+        bring_back(t, 3, done[3], scalar_copy)
+        bring_back(t, 1, done[1], vector_copy)
+        bring_back(t, 2, done[2], vector_copy)
+        bring_back(t, 0, done[0], scalar_half)

@@ -21,6 +21,7 @@ PASS_WORDS = K_PASS // 2
 CH_TILES = A // P
 LOAD_TILES = 2
 HALF_COLS = A // 2
+AHEAD = 3
 LN_2 = math.log(2.0)
 TINY = 2.0 ** -60
 
@@ -68,10 +69,9 @@ def tile_rwkvtimemix_pa_kernel(
         bb_sb = keep.tile([P, ROW_TILES, A], BF16)
         pp_sb = keep.tile([P, ROW_TILES, A], BF16)
 
-        def load_state_half(half):
+        def load_state_half(half, state_sb, state):
             cols = slice(half * HALF_COLS, (half + 1) * HALF_COLS)
-            for state_sb, state in ((bb_sb, bb), (pp_sb, pp), (aa_sb, aa)):
-                nc.sync.dma_start(out=state_sb[:, :, cols], in_=rows_on_partitions(state)[:, :, cols])
+            nc.sync.dma_start(out=state_sb[:, :, cols], in_=rows_on_partitions(state)[:, :, cols])
 
         def load_weights(n):
             channels = slice(n * LOAD_TILES * P, (n + 1) * LOAD_TILES * P)
@@ -82,9 +82,12 @@ def tile_rwkvtimemix_pa_kernel(
                 loaded.append(w_sb)
             return loaded
 
+        for half in range(2):
+            load_state_half(half, bb_sb, bb)
         w_sb = [load_weights(0)]
-        load_state_half(0)
-        load_state_half(1)
+        for half in range(2):
+            load_state_half(half, pp_sb, pp)
+            load_state_half(half, aa_sb, aa)
         for n in range(1, CH_TILES // LOAD_TILES):
             w_sb.append(load_weights(n))
 
@@ -99,20 +102,16 @@ def tile_rwkvtimemix_pa_kernel(
         identity_bf16 = const.tile([P, P], BF16)
         nc.vector.tensor_copy(out=identity_bf16[:], in_=identity[:])
         mix = const.tile([P, 2, 8], F32)
-        one_minus_mix = const.tile([P, 2, 8], F32)
         vec_cols = const.tile([P, 2 * CH_TILES], F32)
         half_both = const.tile([P, CH_TILES], F32)
 
-        order_kept = {mybir.EngineType.DVE, mybir.EngineType.Activation, mybir.EngineType.PE}
+        order_kept = {mybir.EngineType.DVE, mybir.EngineType.Activation, mybir.EngineType.PE, mybir.EngineType.Pool}
         stack.enter_context(tc.manual_schedule(engines=order_kept))
 
         mix_turned = banks.tile([P, 2, P], F32, tag="turned")
         for u in range(2):
             nc.tensor.transpose(mix_turned[:, u, :], mix_rows[:].bitcast(F32)[:, every_second_word(0, u)], identity[:])
         nc.vector.tensor_copy(out=mix[:], in_=mix_turned[:, :, 0:4].bitcast(BF16))
-        nc.vector.tensor_scalar(
-            out=one_minus_mix[:], in0=mix[:], scalar1=-1.0, scalar2=1.0, op0=ALU.mult, op1=ALU.add
-        )
 
         vec_turned = banks.tile([P, P], BF16, tag="turned")
         nc.tensor.transpose(vec_turned[:], vec_rows[:], identity_bf16[:])
@@ -130,45 +129,21 @@ def tile_rwkvtimemix_pa_kernel(
         def regroup(copy, mixed, grouped, g):
             copy(
                 out=grouped[:, g].rearrange("p (c i) t -> p c t i", i=4),
-                in_=mixed[:, g].rearrange("p t (c i) -> p c t i", i=4),
+                in_=mixed[:].rearrange("p t (c i) -> p c t i", i=4),
             )
 
-        xk_mixed = front.tile([P, PASSES, 4, B], BF16)
-        xv_mixed = front.tile([P, PASSES, 4, B], BF16)
-        xk_grouped = front.tile([P, PASSES, B, 4], BF16, align_bytes=64)
-        xv_grouped = front.tile([P, PASSES, B, 4], BF16, align_bytes=64)
-        for g in range(PASSES):
-            for u in range(2):
-                x_turned = banks.tile([P, B], F32, tag="out")
-                alpha_turned = banks.tile([P, B], F32, tag="state")
-                for act_turned, act_sb in ((alpha_turned, alpha_sb), (x_turned, x_sb)):
-                    for r in range(ROW_TILES):
-                        nc.tensor.transpose(
-                            act_turned[:, r * P : (r + 1) * P],
-                            act_sb[:, r, :].bitcast(F32)[:, every_second_word(g, u)], identity[:],
-                        )
-                x_pairs = x_turned[:].bitcast(BF16).rearrange("p (b e) -> p b e", e=2)
-                alpha_pairs = alpha_turned[:].bitcast(BF16).rearrange("p (b e) -> p b e", e=2)
-                for e in range(2):
-                    for first_row, mixed in ((0, xk_mixed), (2, xv_mixed)):
-                        col = 2 * (first_row + g) + e
-                        alpha_part = front.tile([P, B], F32, tag="alpha_part", bufs=4)
-                        nc.scalar.activation(
-                            out=alpha_part[:], in_=alpha_pairs[:, :, e], func=ACT.Copy,
-                            scale=one_minus_mix[:, u, col : col + 1],
-                        )
-                        nc.vector.scalar_tensor_tensor(
-                            out=mixed[:, g, 2 * u + e, :], in0=x_pairs[:, :, e], scalar=mix[:, u, col : col + 1],
-                            in1=alpha_part[:], op0=ALU.mult, op1=ALU.add,
-                        )
-            regroup(nc.vector.tensor_copy, xk_mixed, xk_grouped, g)
-            regroup(nc.vector.tensor_copy, xv_mixed, xv_grouped, g)
-        for grouped, words, scales in ((xk_grouped, xk_words, xk_scales), (xv_grouped, xv_words, xv_scales)):
-            for g in range(PASSES):
-                nc.vector.quantize_mx(
-                    out=words[:, g, :].bitcast(FP8X4), scales=scales[:, g, :],
-                    in_=grouped[:, g].rearrange("p b t -> p (b t)"),
+        log_bb = keep.tile([P, CH_TILES, B], F32)
+
+        def turn_state(out, state_sb, t):
+            for r in range(ROW_TILES):
+                nc.tensor.transpose(
+                    out[:, r * P : (r + 1) * P], state_sb[:, r, tile_channels(t)], identity_bf16[:]
                 )
+
+        def logarithm(t):
+            bb_turned = banks.tile([P, B], BF16, tag="turned")
+            turn_state(bb_turned, bb_sb, t)
+            nc.scalar.activation(out=log_bb[:, t, :], in_=bb_turned[:], func=ACT.Ln, bias=tiny[:])
 
         def turn_weights(t, which, copy):
             tag = ("wk", "wv")[which]
@@ -194,6 +169,61 @@ def tile_rwkvtimemix_pa_kernel(
             )
             return words, scales
 
+        diff = front.tile([P, PASSES, ROW_TILES, 4, P], F32)
+        for g, engine in ((0, nc.vector), (1, nc.gpsimd)):
+            for r in range(ROW_TILES):
+                h_cols = slice(g * K_PASS, (g + 1) * K_PASS)
+                engine.tensor_tensor(
+                    out=diff[:, g, r], in0=x_sb[:, r, h_cols].rearrange("p (j t) -> p t j", t=4),
+                    in1=alpha_sb[:, r, h_cols].rearrange("p (j t) -> p t j", t=4), op=ALU.subtract,
+                )
+        alpha_words = front.tile([P, PASSES, 2, B], F32)
+
+        def turn_alpha(g):
+            for u in range(2):
+                alpha_turned = banks.tile([P, B], F32, tag="state")
+                for r in range(ROW_TILES):
+                    nc.tensor.transpose(
+                        alpha_turned[:, r * P : (r + 1) * P],
+                        alpha_sb[:, r, :].bitcast(F32)[:, every_second_word(g, u)], identity[:],
+                    )
+                nc.scalar.copy(out=alpha_words[:, g, u, :], in_=alpha_turned[:])
+
+        xk_grouped = front.tile([P, PASSES, B, 4], BF16, align_bytes=64)
+        xv_grouped = front.tile([P, PASSES, B, 4], BF16, align_bytes=64)
+        turn_alpha(0)
+        fillers = {(0, 3): (0, 1), (1, 0): (2, 3), (1, 1): (4, 5), (1, 2): (6, 7)}
+        for g in range(PASSES):
+            xk_mixed = front.tile([P, 4, B], BF16, tag="xk_mixed")
+            xv_mixed = front.tile([P, 4, B], BF16, tag="xv_mixed")
+            for t in range(4):
+                diff_turned = banks.tile([P, B], F32, tag="out")
+                for r in range(ROW_TILES):
+                    nc.tensor.transpose(diff_turned[:, r * P : (r + 1) * P], diff[:, g, r, t, :], identity[:])
+                u, e = divmod(t, 2)
+                alpha_part = alpha_words[:, g, u, :].bitcast(BF16).rearrange("p (b e) -> p b e", e=2)[:, :, e]
+                for first_row, mixed in ((0, xk_mixed), (2, xv_mixed)):
+                    col = 2 * (first_row + g) + e
+                    nc.vector.scalar_tensor_tensor(
+                        out=mixed[:, t, :], in0=diff_turned[:], scalar=mix[:, u, col : col + 1], in1=alpha_part,
+                        op0=ALU.mult, op1=ALU.add,
+                    )
+                if (g, t) == (0, 3):
+                    turn_alpha(1)
+                for j in fillers.get((g, t), ()):
+                    logarithm(j)
+            regroup(nc.vector.tensor_copy, xk_mixed, xk_grouped, g)
+            regroup(nc.vector.tensor_copy, xv_mixed, xv_grouped, g)
+            if g == PASSES - 1:
+                weights = [turn_weights(0, which, nc.scalar.copy) for which in range(2)]
+                wk = quantise_weights(weights[0], "wk")
+                wv = quantise_weights(weights[1], "wv")
+            for grouped, words, scales in ((xk_grouped, xk_words, xk_scales), (xv_grouped, xv_words, xv_scales)):
+                nc.vector.quantize_mx(
+                    out=words[:, g, :].bitcast(FP8X4), scales=scales[:, g, :],
+                    in_=grouped[:, g].rearrange("p b t -> p (b t)"),
+                )
+
         def project(weights, x_words, x_scales, tag):
             words, scales = weights
             acc = banks.tile([P, B], F32, tag=tag, bufs=1)
@@ -205,12 +235,6 @@ def tile_rwkvtimemix_pa_kernel(
                     start=(g == 0), stop=(g == PASSES - 1),
                 )
             return acc
-
-        def turn_state(out, state_sb, t):
-            for r in range(ROW_TILES):
-                nc.tensor.transpose(
-                    out[:, r * P : (r + 1) * P], state_sb[:, r, tile_channels(t)], identity_bf16[:]
-                )
 
         def turn_aa_bb(t):
             turned = banks.tile([P, 2, B], BF16, tag="state")
@@ -232,10 +256,8 @@ def tile_rwkvtimemix_pa_kernel(
             tile = late.tile([P, B], F32, tag=tag)
             return tile
 
-        log_bb = keep.tile([P, CH_TILES, B], F32)
-
         def two_over_bb(t):
-            two_rho = late_tile("two_rho")
+            two_rho = late.tile([P, B], F32, tag="two_rho", bufs=AHEAD + 2)
             nc.scalar.activation(out=two_rho[:], in_=log_bb[:, t, :], func=ACT.Exp, scale=-1.0, bias=ln_2[:])
             return two_rho
 
@@ -271,24 +293,18 @@ def tile_rwkvtimemix_pa_kernel(
         def vector_copy(dst, src):
             nc.vector.tensor_copy(out=dst, in_=src)
 
-        grouped = [[turn_weights(0, 0, nc.scalar.copy), turn_weights(0, 1, nc.scalar.copy)]]
-        wk = quantise_weights(grouped[0][0], "wk")
-        wv = quantise_weights(grouped[0][1], "wv")
-        for t in range(CH_TILES):
-            bb_turned = banks.tile([P, B], BF16, tag="out")
-            turn_state(bb_turned, bb_sb, t)
-            nc.scalar.activation(out=log_bb[:, t, :], in_=bb_turned[:], func=ACT.Ln, bias=tiny[:])
-        state = turn_aa_bb(0)
         pp_t = copy_pp(turn_pp(0))
-        two_rho = two_over_bb(0)
-        grouped.append([turn_weights(1, 0, nc.scalar.copy), turn_weights(1, 1, nc.scalar.copy)])
+        grouped = [weights, [turn_weights(1, which, nc.scalar.copy) for which in range(2)]]
+        state = turn_aa_bb(0)
         k_ps = project(wk, xk_words, xk_scales, "k")
         v_ps = project(wv, xv_words, xv_scales, "v")
+        two_rhos = [two_over_bb(t) for t in range(AHEAD)]
 
         done = None
         for t in range(CH_TILES):
             more = t + 1 < CH_TILES
             decay = vec_cols[:, t : t + 1]
+            two_rho = two_rhos[t]
             if more:
                 next_state = turn_aa_bb(t + 1)
                 next_pp = turn_pp(t + 1)
@@ -299,11 +315,17 @@ def tile_rwkvtimemix_pa_kernel(
             )
             grow_new = late_tile("grow_new")
             nc.scalar.activation(out=grow_new[:], in_=d2[:], func=ACT.Exp)
+            qq2 = late_tile("qq2")
+            nc.vector.scalar_tensor_tensor(
+                out=qq2[:], in0=pp_t[:], scalar=decay, in1=k_ps[:], op0=ALU.add, op1=ALU.max
+            )
             nc.vector.tensor_tensor(out=two_rho[:], in0=state[:, 0, :], in1=two_rho[:], op=ALU.mult)
             gate = late_tile("gate")
             nc.vector.tensor_tensor(out=gate[:], in0=d2[:], in1=log_bb[:, t, :], op=ALU.subtract)
             grow_old = late_tile("grow_old")
             nc.scalar.activation(out=grow_old[:], in_=d2[:], func=ACT.Exp, scale=-1.0)
+            if more:
+                wk = quantise_weights(grouped[t + 1][0], "wk")
             swing = late_tile("swing")
             nc.vector.scalar_tensor_tensor(
                 out=swing[:], in0=two_rho[:], scalar=-0.5, in1=v_ps[:], op0=ALU.mult, op1=ALU.add
@@ -313,12 +335,7 @@ def tile_rwkvtimemix_pa_kernel(
             nc.scalar.activation(
                 out=gate[:], in_=gate[:], func=ACT.Tanh, scale=0.5, bias=half_both[:, t : t + 1]
             )
-            qq2 = late_tile("qq2")
-            nc.vector.scalar_tensor_tensor(
-                out=qq2[:], in0=pp_t[:], scalar=decay, in1=k_ps[:], op0=ALU.add, op1=ALU.max
-            )
             if more:
-                wk = quantise_weights(grouped[t + 1][0], "wk")
                 wv = quantise_weights(grouped[t + 1][1], "wv")
 
             if done is not None:
@@ -326,11 +343,13 @@ def tile_rwkvtimemix_pa_kernel(
                 bring_back(t - 1, 1, done[1], scalar_copy)
             if t + 2 < CH_TILES:
                 grouped.append([turn_weights(t + 2, 0, nc.scalar.copy), turn_weights(t + 2, 1, nc.scalar.copy)])
+            if more:
+                k_ps = project(wk, xk_words, xk_scales, "k")
             if done is not None:
                 bring_back(t - 1, 2, done[2], scalar_copy)
                 bring_back(t - 1, 0, done[0], scalar_half)
-            if more:
-                next_two_rho = two_over_bb(t + 1)
+            if t + AHEAD < CH_TILES:
+                two_rhos.append(two_over_bb(t + AHEAD))
 
             e2b = late_tile("e2b")
             nc.vector.tensor_scalar(out=e2b[:], in0=grow_new[:], scalar1=1.0, scalar2=None, op0=ALU.min)
@@ -349,9 +368,8 @@ def tile_rwkvtimemix_pa_kernel(
             )
             done = ((two_rho, swing), (old_aa, new_aa), (old_bb, e2b), (qq2,))
             if more:
-                k_ps = project(wk, xk_words, xk_scales, "k")
                 v_ps = project(wv, xv_words, xv_scales, "v")
-                state, pp_t, two_rho = next_state, next_pp_t, next_two_rho
+                state, pp_t = next_state, next_pp_t
         bring_back(t, 3, done[3], scalar_copy)
         bring_back(t, 1, done[1], vector_copy)
         bring_back(t, 2, done[2], vector_copy)

@@ -20,7 +20,7 @@ PASSES = H // K_PASS
 PASS_WORDS = K_PASS // 2
 CH_TILES = A // P
 LOAD_TILES = 2
-HALF_COLS = A // 2
+ALONE_FROM = 4
 AHEAD = 3
 LN_2 = math.log(2.0)
 TINY = 2.0 ** -60
@@ -42,7 +42,7 @@ def tile_rwkvtimemix_pa_kernel(
         banks = stack.enter_context(tc.psum_pool(name="banks", bufs=2))
 
         def rows_on_partitions(dram):
-            return dram.rearrange("(r p) n -> p r n", p=P)
+            return dram.rearrange("(p r) n -> p r n", p=P)
 
         def every_second_word(g, u):
             return slice(g * PASS_WORDS + u, (g + 1) * PASS_WORDS, 2)
@@ -56,22 +56,29 @@ def tile_rwkvtimemix_pa_kernel(
         nc.gpsimd.memset(vec_rows[:], 0.0)
         nc.sync.dma_start(out=mix_rows[0:2, :], in_=time_mix_k.rearrange("(j c) -> j c", c=K_PASS))
         nc.sync.dma_start(out=mix_rows[2:4, :], in_=time_mix_v.rearrange("(j c) -> j c", c=K_PASS))
-        x_sb = keep.tile([P, ROW_TILES, H], BF16)
-        alpha_sb = keep.tile([P, ROW_TILES, H], BF16)
+        alpha_pieces = []
+        x_pieces = []
+        for g in range(PASSES):
+            for half in range(2):
+                slots = slice(2 * half, 2 * half + 2)
+                h_cols = slice(g * K_PASS, (g + 1) * K_PASS)
+                for pieces, act, name in ((alpha_pieces, alpha, "alpha"), (x_pieces, x, "x")):
+                    piece = keep.tile([P, 2, K_PASS], BF16, name="%s_%d_%d" % (name, g, half))
+                    nc.sync.dma_start(out=piece[:], in_=rows_on_partitions(act)[:, slots, h_cols])
+                    pieces.append(piece)
+
+        def rows_of_slot(pieces, g, r):
+            return pieces[2 * g + r // 2][:, r % 2, :]
+
+
         nc.sync.dma_start(out=vec_rows[0:CH_TILES, :], in_=time_decay.rearrange("(j c) -> j c", c=P))
         nc.sync.dma_start(out=vec_rows[CH_TILES : 2 * CH_TILES, :], in_=time_first.rearrange("(j c) -> j c", c=P))
-        for g in range(PASSES):
-            h_cols = slice(g * K_PASS, (g + 1) * K_PASS)
-            nc.sync.dma_start(out=x_sb[:, :, h_cols], in_=rows_on_partitions(x)[:, :, h_cols])
-            nc.sync.dma_start(out=alpha_sb[:, :, h_cols], in_=rows_on_partitions(alpha)[:, :, h_cols])
-
         aa_sb = keep.tile([P, ROW_TILES, A], BF16)
         bb_sb = keep.tile([P, ROW_TILES, A], BF16)
         pp_sb = keep.tile([P, ROW_TILES, A], BF16)
 
-        def load_state_half(half, state_sb, state):
-            cols = slice(half * HALF_COLS, (half + 1) * HALF_COLS)
-            nc.sync.dma_start(out=state_sb[:, :, cols], in_=rows_on_partitions(state)[:, :, cols])
+        def load_state(state_sb, state):
+            nc.sync.dma_start(out=state_sb[:], in_=rows_on_partitions(state))
 
         def load_weights(n):
             channels = slice(n * LOAD_TILES * P, (n + 1) * LOAD_TILES * P)
@@ -82,12 +89,10 @@ def tile_rwkvtimemix_pa_kernel(
                 loaded.append(w_sb)
             return loaded
 
-        for half in range(2):
-            load_state_half(half, bb_sb, bb)
+        load_state(bb_sb, bb)
         w_sb = [load_weights(0)]
-        for half in range(2):
-            load_state_half(half, pp_sb, pp)
-            load_state_half(half, aa_sb, aa)
+        load_state(pp_sb, pp)
+        load_state(aa_sb, aa)
         for n in range(1, CH_TILES // LOAD_TILES):
             w_sb.append(load_weights(n))
 
@@ -113,14 +118,6 @@ def tile_rwkvtimemix_pa_kernel(
             nc.tensor.transpose(mix_turned[:, u, :], mix_rows[:].bitcast(F32)[:, every_second_word(0, u)], identity[:])
         nc.vector.tensor_copy(out=mix[:], in_=mix_turned[:, :, 0:4].bitcast(BF16))
 
-        vec_turned = banks.tile([P, P], BF16, tag="turned")
-        nc.tensor.transpose(vec_turned[:], vec_rows[:], identity_bf16[:])
-        nc.vector.tensor_copy(out=vec_cols[:], in_=vec_turned[:, 0 : 2 * CH_TILES])
-        nc.vector.tensor_tensor(
-            out=half_both[:], in0=vec_cols[:, 0:CH_TILES], in1=vec_cols[:, CH_TILES : 2 * CH_TILES], op=ALU.add
-        )
-        nc.vector.tensor_scalar(out=half_both[:], in0=half_both[:], scalar1=0.5, scalar2=None, op0=ALU.mult)
-
         xk_words = keep.tile([P, PASSES, B], U32, align_bytes=64)
         xk_scales = keep.tile([P, PASSES, B], U8, align_bytes=64)
         xv_words = keep.tile([P, PASSES, B], U32, align_bytes=64)
@@ -141,7 +138,8 @@ def tile_rwkvtimemix_pa_kernel(
                 )
 
         def logarithm(t):
-            bb_turned = banks.tile([P, B], BF16, tag="turned")
+            tag, bufs = (("turned", 2), ("turned", 2), ("k", 1), ("v", 1))[t % 4]
+            bb_turned = banks.tile([P, B], BF16, tag=tag, bufs=bufs)
             turn_state(bb_turned, bb_sb, t)
             nc.scalar.activation(out=log_bb[:, t, :], in_=bb_turned[:], func=ACT.Ln, bias=tiny[:])
 
@@ -172,35 +170,35 @@ def tile_rwkvtimemix_pa_kernel(
         diff = front.tile([P, PASSES, ROW_TILES, 4, P], F32)
         for g, engine in ((0, nc.vector), (1, nc.gpsimd)):
             for r in range(ROW_TILES):
-                h_cols = slice(g * K_PASS, (g + 1) * K_PASS)
                 engine.tensor_tensor(
-                    out=diff[:, g, r], in0=x_sb[:, r, h_cols].rearrange("p (j t) -> p t j", t=4),
-                    in1=alpha_sb[:, r, h_cols].rearrange("p (j t) -> p t j", t=4), op=ALU.subtract,
+                    out=diff[:, g, r], in0=rows_of_slot(x_pieces, g, r).rearrange("p (j t) -> p t j", t=4),
+                    in1=rows_of_slot(alpha_pieces, g, r).rearrange("p (j t) -> p t j", t=4), op=ALU.subtract,
                 )
         alpha_words = front.tile([P, PASSES, 2, B], F32)
 
-        def turn_alpha(g):
-            for u in range(2):
-                alpha_turned = banks.tile([P, B], F32, tag="state")
-                for r in range(ROW_TILES):
-                    nc.tensor.transpose(
-                        alpha_turned[:, r * P : (r + 1) * P],
-                        alpha_sb[:, r, :].bitcast(F32)[:, every_second_word(g, u)], identity[:],
-                    )
-                nc.scalar.copy(out=alpha_words[:, g, u, :], in_=alpha_turned[:])
+        def turn_alpha(g, u):
+            alpha_turned = banks.tile([P, B], F32, tag="state")
+            for r in range(ROW_TILES):
+                nc.tensor.transpose(
+                    alpha_turned[:, r * P : (r + 1) * P],
+                    rows_of_slot(alpha_pieces, g, r).bitcast(F32)[:, every_second_word(0, u)], identity[:],
+                )
+            nc.scalar.copy(out=alpha_words[:, g, u, :], in_=alpha_turned[:])
 
         xk_grouped = front.tile([P, PASSES, B, 4], BF16, align_bytes=64)
         xv_grouped = front.tile([P, PASSES, B, 4], BF16, align_bytes=64)
-        turn_alpha(0)
-        fillers = {(0, 3): (0, 1), (1, 0): (2, 3), (1, 1): (4, 5), (1, 2): (6, 7)}
+        fillers = {(0, 3): (0, 1), (1, 0): (2, 3, 4), (1, 1): (5, 6, 7)}
         for g in range(PASSES):
             xk_mixed = front.tile([P, 4, B], BF16, tag="xk_mixed")
             xv_mixed = front.tile([P, 4, B], BF16, tag="xv_mixed")
             for t in range(4):
+                u, e = divmod(t, 2)
+                if t == 0:
+                    turn_alpha(g, 0)
+                    turn_alpha(g, 1)
                 diff_turned = banks.tile([P, B], F32, tag="out")
                 for r in range(ROW_TILES):
                     nc.tensor.transpose(diff_turned[:, r * P : (r + 1) * P], diff[:, g, r, t, :], identity[:])
-                u, e = divmod(t, 2)
                 alpha_part = alpha_words[:, g, u, :].bitcast(BF16).rearrange("p (b e) -> p b e", e=2)[:, :, e]
                 for first_row, mixed in ((0, xk_mixed), (2, xv_mixed)):
                     col = 2 * (first_row + g) + e
@@ -208,16 +206,23 @@ def tile_rwkvtimemix_pa_kernel(
                         out=mixed[:, t, :], in0=diff_turned[:], scalar=mix[:, u, col : col + 1], in1=alpha_part,
                         op0=ALU.mult, op1=ALU.add,
                     )
-                if (g, t) == (0, 3):
-                    turn_alpha(1)
                 for j in fillers.get((g, t), ()):
                     logarithm(j)
+                if (g, t) == (1, 2):
+                    weights = [turn_weights(0, which, nc.scalar.copy) for which in range(2)]
+                if (g, t) == (1, 3):
+                    wk = quantise_weights(weights[0], "wk")
+                    wv = quantise_weights(weights[1], "wv")
             regroup(nc.vector.tensor_copy, xk_mixed, xk_grouped, g)
             regroup(nc.vector.tensor_copy, xv_mixed, xv_grouped, g)
-            if g == PASSES - 1:
-                weights = [turn_weights(0, which, nc.scalar.copy) for which in range(2)]
-                wk = quantise_weights(weights[0], "wk")
-                wv = quantise_weights(weights[1], "wv")
+            if g == 0:
+                vec_turned = banks.tile([P, P], BF16, tag="turned")
+                nc.tensor.transpose(vec_turned[:], vec_rows[:], identity_bf16[:])
+                nc.vector.tensor_copy(out=vec_cols[:], in_=vec_turned[:, 0 : 2 * CH_TILES])
+                nc.vector.tensor_tensor(
+                    out=half_both[:], in0=vec_cols[:, 0:CH_TILES], in1=vec_cols[:, CH_TILES : 2 * CH_TILES], op=ALU.add
+                )
+                nc.vector.tensor_scalar(out=half_both[:], in0=half_both[:], scalar1=0.5, scalar2=None, op0=ALU.mult)
             for grouped, words, scales in ((xk_grouped, xk_words, xk_scales), (xv_grouped, xv_words, xv_scales)):
                 nc.vector.quantize_mx(
                     out=words[:, g, :].bitcast(FP8X4), scales=scales[:, g, :],
@@ -263,26 +268,27 @@ def tile_rwkvtimemix_pa_kernel(
 
         results = {}
 
-        def bring_back(t, out, sources, copy):
+        def bring_back(t, out, sources, copy, tag="out"):
             n, i = divmod(t, LOAD_TILES)
-            turned = banks.tile([P, ROW_TILES, P], F32, tag="out")
+            turned = banks.tile([P, ROW_TILES, P], F32, tag=tag)
             for r in range(ROW_TILES):
                 for s, source in enumerate(sources):
                     nc.tensor.matmul(
                         out=turned[:, r, :], lhsT=source[:, r * P : (r + 1) * P], rhs=identity[:],
                         start=(s == 0), stop=(s == len(sources) - 1), is_transpose=True,
                     )
-            if (out, n) not in results:
-                result = late.tile([P, ROW_TILES, LOAD_TILES * P], F32, tag="out_%d" % out)
-                results[(out, n)] = result
-            result = results[(out, n)]
-            cols = slice(i * P, (i + 1) * P)
-            copy(result[:, :, cols], turned[:])
             dram = rows_on_partitions((out_0, out_1, out_2, out_3)[out])
-            if n == CH_TILES // LOAD_TILES - 1:
-                nc.sync.dma_start(out=dram[:, :, tile_channels(t)], in_=result[:, :, cols])
-            elif i == LOAD_TILES - 1:
-                nc.sync.dma_start(out=dram[:, :, n * LOAD_TILES * P : (n + 1) * LOAD_TILES * P], in_=result[:])
+            if t >= ALONE_FROM:
+                result = late.tile([P, ROW_TILES, P], F32, tag="out_%d" % out)
+                copy(result[:], turned[:])
+                nc.sync.dma_start(out=dram[:, :, tile_channels(t)], in_=result[:])
+                return
+            if i == 0:
+                pair = late.tile([P, ROW_TILES, LOAD_TILES * P], F32, tag="out_%d" % out)
+                results[out] = pair
+            copy(results[out][:, :, i * P : (i + 1) * P], turned[:])
+            if i == LOAD_TILES - 1:
+                nc.sync.dma_start(out=dram[:, :, n * LOAD_TILES * P : (n + 1) * LOAD_TILES * P], in_=results[out][:])
 
         def scalar_copy(dst, src):
             nc.scalar.copy(out=dst, in_=src)
@@ -332,22 +338,25 @@ def tile_rwkvtimemix_pa_kernel(
             )
             if more:
                 next_pp_t = copy_pp(next_pp)
-            nc.scalar.activation(
-                out=gate[:], in_=gate[:], func=ACT.Tanh, scale=0.5, bias=half_both[:, t : t + 1]
-            )
             if more:
                 wv = quantise_weights(grouped[t + 1][1], "wv")
 
             if done is not None:
                 bring_back(t - 1, 3, done[3], scalar_copy)
                 bring_back(t - 1, 1, done[1], scalar_copy)
+            nc.scalar.activation(
+                out=gate[:], in_=gate[:], func=ACT.Tanh, scale=0.5, bias=half_both[:, t : t + 1]
+            )
             if t + 2 < CH_TILES:
                 grouped.append([turn_weights(t + 2, 0, nc.scalar.copy), turn_weights(t + 2, 1, nc.scalar.copy)])
             if more:
                 k_ps = project(wk, xk_words, xk_scales, "k")
+            spare = "out" if more else "turned"
             if done is not None:
-                bring_back(t - 1, 2, done[2], scalar_copy)
-                bring_back(t - 1, 0, done[0], scalar_half)
+                bring_back(t - 1, 2, done[2], scalar_copy, spare)
+                bring_back(t - 1, 0, done[0], scalar_half, spare)
+            if not more:
+                bring_back(t, 3, (qq2,), scalar_copy)
             if t + AHEAD < CH_TILES:
                 two_rhos.append(two_over_bb(t + AHEAD))
 
@@ -359,6 +368,8 @@ def tile_rwkvtimemix_pa_kernel(
             )
             new_aa = late_tile("new_aa")
             nc.vector.tensor_tensor(out=new_aa[:], in0=e2b[:], in1=v_ps[:], op=ALU.mult)
+            if not more:
+                bring_back(t, 1, (old_aa, new_aa), scalar_copy)
             old_bb = late_tile("old_bb")
             nc.vector.scalar_tensor_tensor(
                 out=old_bb[:], in0=grow_old[:], scalar=1.0, in1=state[:, 1, :], op0=ALU.min, op1=ALU.mult
@@ -366,11 +377,10 @@ def tile_rwkvtimemix_pa_kernel(
             nc.vector.scalar_tensor_tensor(
                 out=swing[:], in0=gate[:], scalar=1.0, in1=swing[:], op0=ALU.add, op1=ALU.mult
             )
+            if not more:
+                bring_back(t, 2, (old_bb, e2b), vector_copy, spare)
             done = ((two_rho, swing), (old_aa, new_aa), (old_bb, e2b), (qq2,))
             if more:
                 v_ps = project(wv, xv_words, xv_scales, "v")
                 state, pp_t = next_state, next_pp_t
-        bring_back(t, 3, done[3], scalar_copy)
-        bring_back(t, 1, done[1], vector_copy)
-        bring_back(t, 2, done[2], vector_copy)
-        bring_back(t, 0, done[0], scalar_half)
+        bring_back(t, 0, done[0], scalar_half, spare)

import math
from contextlib import ExitStack

import concourse.mybir as mybir
from concourse.masks import make_identity

F32 = mybir.dt.float32
BF16 = mybir.dt.bfloat16
U32 = mybir.dt.uint32
U8 = mybir.dt.uint8
FP8X4 = mybir.dt.float8_e4m3fn_x4
ALU = mybir.AluOpType
ACT = mybir.ActivationFunctionType

B, H, A = 512, 1024, 1024
P = 128
ROW_TILES = B // P
K_PASS = 4 * P
PASSES = H // K_PASS
PASS_WORDS = K_PASS // 2
CH_TILES = A // P
LOAD_TILES = 2
ALONE_FROM = 4
AHEAD = 3
LN_2 = math.log(2.0)
TINY = 2.0 ** -60

FLOPS = 2 * 2 * B * H * A


def tile_rwkvtimemix_pa_kernel(
    tc, x, alpha, aa, bb, pp, time_decay, time_first, time_mix_k, time_mix_v, Wk, Wv,
    out_0, out_1, out_2, out_3,
):
    nc = tc.nc
    with ExitStack() as stack:
        const = stack.enter_context(tc.tile_pool(name="const", bufs=1))
        keep = stack.enter_context(tc.tile_pool(name="keep", bufs=1))
        flow = stack.enter_context(tc.tile_pool(name="flow", bufs=2))
        front = stack.enter_context(tc.tile_pool(name="front", bufs=1))
        late = stack.enter_context(tc.tile_pool(name="late", bufs=2))
        banks = stack.enter_context(tc.psum_pool(name="banks", bufs=2))

        def rows_on_partitions(dram):
            return dram.rearrange("(p r) n -> p r n", p=P)

        def every_second_word(g, u):
            return slice(g * PASS_WORDS + u, (g + 1) * PASS_WORDS, 2)

        def tile_channels(t):
            return slice(t * P, (t + 1) * P)

        mix_rows = const.tile([P, K_PASS], BF16)
        nc.gpsimd.memset(mix_rows[:], 0.0)
        vec_rows = const.tile([P, P], BF16)
        nc.gpsimd.memset(vec_rows[:], 0.0)
        nc.sync.dma_start(out=mix_rows[0:2, :], in_=time_mix_k.rearrange("(j c) -> j c", c=K_PASS))
        nc.sync.dma_start(out=mix_rows[2:4, :], in_=time_mix_v.rearrange("(j c) -> j c", c=K_PASS))
        alpha_pieces = []
        x_pieces = []
        for g in range(PASSES):
            for half in range(2):
                slots = slice(2 * half, 2 * half + 2)
                h_cols = slice(g * K_PASS, (g + 1) * K_PASS)
                for pieces, act, name in ((alpha_pieces, alpha, "alpha"), (x_pieces, x, "x")):
                    piece = keep.tile([P, 2, K_PASS], BF16, name="%s_%d_%d" % (name, g, half))
                    nc.sync.dma_start(out=piece[:], in_=rows_on_partitions(act)[:, slots, h_cols])
                    pieces.append(piece)

        def rows_of_slot(pieces, g, r):
            return pieces[2 * g + r // 2][:, r % 2, :]


        nc.sync.dma_start(out=vec_rows[0:CH_TILES, :], in_=time_decay.rearrange("(j c) -> j c", c=P))
        nc.sync.dma_start(out=vec_rows[CH_TILES : 2 * CH_TILES, :], in_=time_first.rearrange("(j c) -> j c", c=P))
        aa_sb = keep.tile([P, ROW_TILES, A], BF16)
        bb_sb = keep.tile([P, ROW_TILES, A], BF16)
        pp_sb = keep.tile([P, ROW_TILES, A], BF16)

        def load_state(state_sb, state):
            nc.sync.dma_start(out=state_sb[:], in_=rows_on_partitions(state))

        def load_weights(n):
            channels = slice(n * LOAD_TILES * P, (n + 1) * LOAD_TILES * P)
            loaded = []
            for w, tag in ((Wk, "wk"), (Wv, "wv")):
                w_sb = flow.tile([P, LOAD_TILES, H], BF16, tag=tag)
                nc.sync.dma_start(out=w_sb[:], in_=w[channels, :].rearrange("(i p) n -> p i n", p=P))
                loaded.append(w_sb)
            return loaded

        load_state(bb_sb, bb)
        w_sb = [load_weights(0)]
        load_state(pp_sb, pp)
        load_state(aa_sb, aa)
        for n in range(1, CH_TILES // LOAD_TILES):
            w_sb.append(load_weights(n))

        tiny = const.tile([P, 1], F32)
        nc.vector.memset(tiny[:], TINY)
        warm = const.tile([P, 1], F32)
        nc.scalar.activation(out=warm[:], in_=tiny[:], func=ACT.Ln)
        ln_2 = const.tile([P, 1], F32)
        nc.vector.tensor_scalar(out=ln_2[:], in0=tiny[:], scalar1=0.0, scalar2=LN_2, op0=ALU.mult, op1=ALU.add)
        identity = const.tile([P, P], F32)
        make_identity(nc, identity[:])
        identity_bf16 = const.tile([P, P], BF16)
        nc.vector.tensor_copy(out=identity_bf16[:], in_=identity[:])
        mix = const.tile([P, 2, 8], F32)
        vec_cols = const.tile([P, 2 * CH_TILES], F32)
        half_both = const.tile([P, CH_TILES], F32)

        order_kept = {mybir.EngineType.DVE, mybir.EngineType.Activation, mybir.EngineType.PE, mybir.EngineType.Pool}
        stack.enter_context(tc.manual_schedule(engines=order_kept))

        mix_turned = banks.tile([P, 2, P], F32, tag="turned")
        for u in range(2):
            nc.tensor.transpose(mix_turned[:, u, :], mix_rows[:].bitcast(F32)[:, every_second_word(0, u)], identity[:])
        nc.vector.tensor_copy(out=mix[:], in_=mix_turned[:, :, 0:4].bitcast(BF16))

        xk_words = keep.tile([P, PASSES, B], U32, align_bytes=64)
        xk_scales = keep.tile([P, PASSES, B], U8, align_bytes=64)
        xv_words = keep.tile([P, PASSES, B], U32, align_bytes=64)
        xv_scales = keep.tile([P, PASSES, B], U8, align_bytes=64)

        def regroup(copy, mixed, grouped, g):
            copy(
                out=grouped[:, g].rearrange("p (c i) t -> p c t i", i=4),
                in_=mixed[:].rearrange("p t (c i) -> p c t i", i=4),
            )

        log_bb = keep.tile([P, CH_TILES, B], F32)

        def turn_state(out, state_sb, t):
            for r in range(ROW_TILES):
                nc.tensor.transpose(
                    out[:, r * P : (r + 1) * P], state_sb[:, r, tile_channels(t)], identity_bf16[:]
                )

        def logarithm(t):
            tag, bufs = (("turned", 2), ("turned", 2), ("k", 1), ("v", 1))[t % 4]
            bb_turned = banks.tile([P, B], BF16, tag=tag, bufs=bufs)
            turn_state(bb_turned, bb_sb, t)
            nc.scalar.activation(out=log_bb[:, t, :], in_=bb_turned[:], func=ACT.Ln, bias=tiny[:])

        def turn_weights(t, which, copy):
            tag = ("wk", "wv")[which]
            words = w_sb[t // LOAD_TILES][which][:, t % LOAD_TILES, :].bitcast(F32)
            grouped = flow.tile([P, PASSES, 4 * P], BF16, tag=tag + "_grouped", align_bytes=64)
            w_turned = banks.tile([P, PASSES, 2, P], F32, tag="turned")
            for g in range(PASSES):
                for u in range(2):
                    nc.tensor.transpose(w_turned[:, g, u, :], words[:, every_second_word(g, u)], identity[:])
            copy(
                out=grouped[:].bitcast(F32).rearrange("p g (a u) -> p g a u", u=2),
                in_=w_turned[:].rearrange("p g u a -> p g a u"),
            )
            return grouped

        def quantise_weights(grouped, tag):
            words = flow.tile([P, PASSES, P], U32, tag=tag + "_words", align_bytes=64)
            scales = flow.tile([P, PASSES, P], U8, tag=tag + "_scales", align_bytes=64)
            nc.vector.quantize_mx(
                out=words[:].rearrange("p g a -> p (g a)").bitcast(FP8X4),
                scales=scales[:].rearrange("p g a -> p (g a)"),
                in_=grouped[:].rearrange("p g a -> p (g a)"),
            )
            return words, scales

        diff = front.tile([P, PASSES, ROW_TILES, 4, P], F32)
        for g, engine in ((0, nc.vector), (1, nc.gpsimd)):
            for r in range(ROW_TILES):
                engine.tensor_tensor(
                    out=diff[:, g, r], in0=rows_of_slot(x_pieces, g, r).rearrange("p (j t) -> p t j", t=4),
                    in1=rows_of_slot(alpha_pieces, g, r).rearrange("p (j t) -> p t j", t=4), op=ALU.subtract,
                )
        alpha_words = front.tile([P, PASSES, 2, B], F32)

        def turn_alpha(g, u):
            alpha_turned = banks.tile([P, B], F32, tag="state")
            for r in range(ROW_TILES):
                nc.tensor.transpose(
                    alpha_turned[:, r * P : (r + 1) * P],
                    rows_of_slot(alpha_pieces, g, r).bitcast(F32)[:, every_second_word(0, u)], identity[:],
                )
            nc.scalar.copy(out=alpha_words[:, g, u, :], in_=alpha_turned[:])

        xk_grouped = front.tile([P, PASSES, B, 4], BF16, align_bytes=64)
        xv_grouped = front.tile([P, PASSES, B, 4], BF16, align_bytes=64)
        fillers = {(0, 3): (0, 1), (1, 0): (2, 3, 4), (1, 1): (5, 6, 7)}
        for g in range(PASSES):
            xk_mixed = front.tile([P, 4, B], BF16, tag="xk_mixed")
            xv_mixed = front.tile([P, 4, B], BF16, tag="xv_mixed")
            for t in range(4):
                u, e = divmod(t, 2)
                if t == 0:
                    turn_alpha(g, 0)
                    turn_alpha(g, 1)
                diff_turned = banks.tile([P, B], F32, tag="out")
                for r in range(ROW_TILES):
                    nc.tensor.transpose(diff_turned[:, r * P : (r + 1) * P], diff[:, g, r, t, :], identity[:])
                alpha_part = alpha_words[:, g, u, :].bitcast(BF16).rearrange("p (b e) -> p b e", e=2)[:, :, e]
                for first_row, mixed in ((0, xk_mixed), (2, xv_mixed)):
                    col = 2 * (first_row + g) + e
                    nc.vector.scalar_tensor_tensor(
                        out=mixed[:, t, :], in0=diff_turned[:], scalar=mix[:, u, col : col + 1], in1=alpha_part,
                        op0=ALU.mult, op1=ALU.add,
                    )
                for j in fillers.get((g, t), ()):
                    logarithm(j)
                if (g, t) == (1, 2):
                    weights = [turn_weights(0, which, nc.scalar.copy) for which in range(2)]
                if (g, t) == (1, 3):
                    wk = quantise_weights(weights[0], "wk")
                    wv = quantise_weights(weights[1], "wv")
            regroup(nc.vector.tensor_copy, xk_mixed, xk_grouped, g)
            regroup(nc.vector.tensor_copy, xv_mixed, xv_grouped, g)
            if g == 0:
                vec_turned = banks.tile([P, P], BF16, tag="turned")
                nc.tensor.transpose(vec_turned[:], vec_rows[:], identity_bf16[:])
                nc.vector.tensor_copy(out=vec_cols[:], in_=vec_turned[:, 0 : 2 * CH_TILES])
                nc.vector.tensor_tensor(
                    out=half_both[:], in0=vec_cols[:, 0:CH_TILES], in1=vec_cols[:, CH_TILES : 2 * CH_TILES], op=ALU.add
                )
                nc.vector.tensor_scalar(out=half_both[:], in0=half_both[:], scalar1=0.5, scalar2=None, op0=ALU.mult)
            for grouped, words, scales in ((xk_grouped, xk_words, xk_scales), (xv_grouped, xv_words, xv_scales)):
                nc.vector.quantize_mx(
                    out=words[:, g, :].bitcast(FP8X4), scales=scales[:, g, :],
                    in_=grouped[:, g].rearrange("p b t -> p (b t)"),
                )

        def project(weights, x_words, x_scales, tag):
            words, scales = weights
            acc = banks.tile([P, B], F32, tag=tag, bufs=1)
            for g in range(PASSES):
                nc.tensor.matmul_mx(
                    out=acc[:],
                    lhsT=words[:, g, :].bitcast(FP8X4), lhsT_scale=scales[:, g, :],
                    rhs=x_words[:, g, :].bitcast(FP8X4), rhs_scale=x_scales[:, g, :],
                    start=(g == 0), stop=(g == PASSES - 1),
                )
            return acc

        def turn_aa_bb(t):
            turned = banks.tile([P, 2, B], BF16, tag="state")
            turn_state(turned[:, 0, :], aa_sb, t)
            turn_state(turned[:, 1, :], bb_sb, t)
            return turned

        def turn_pp(t):
            turned = banks.tile([P, B], BF16, tag="turned")
            turn_state(turned, pp_sb, t)
            return turned

        def copy_pp(turned):
            pp_t = flow.tile([P, B], BF16, tag="pp_t")
            nc.scalar.copy(out=pp_t[:], in_=turned[:])
            return pp_t

        def late_tile(tag):
            tile = late.tile([P, B], F32, tag=tag)
            return tile

        def two_over_bb(t):
            two_rho = late.tile([P, B], F32, tag="two_rho", bufs=AHEAD + 2)
            nc.scalar.activation(out=two_rho[:], in_=log_bb[:, t, :], func=ACT.Exp, scale=-1.0, bias=ln_2[:])
            return two_rho

        results = {}

        def bring_back(t, out, sources, copy, tag="out"):
            n, i = divmod(t, LOAD_TILES)
            turned = banks.tile([P, ROW_TILES, P], F32, tag=tag)
            for r in range(ROW_TILES):
                for s, source in enumerate(sources):
                    nc.tensor.matmul(
                        out=turned[:, r, :], lhsT=source[:, r * P : (r + 1) * P], rhs=identity[:],
                        start=(s == 0), stop=(s == len(sources) - 1), is_transpose=True,
                    )
            dram = rows_on_partitions((out_0, out_1, out_2, out_3)[out])
            if t >= ALONE_FROM:
                result = late.tile([P, ROW_TILES, P], F32, tag="out_%d" % out)
                copy(result[:], turned[:])
                nc.sync.dma_start(out=dram[:, :, tile_channels(t)], in_=result[:])
                return
            if i == 0:
                pair = late.tile([P, ROW_TILES, LOAD_TILES * P], F32, tag="out_%d" % out)
                results[out] = pair
            copy(results[out][:, :, i * P : (i + 1) * P], turned[:])
            if i == LOAD_TILES - 1:
                nc.sync.dma_start(out=dram[:, :, n * LOAD_TILES * P : (n + 1) * LOAD_TILES * P], in_=results[out][:])

        def scalar_copy(dst, src):
            nc.scalar.copy(out=dst, in_=src)

        def scalar_half(dst, src):
            nc.scalar.activation(out=dst, in_=src, func=ACT.Copy, scale=0.5)

        def vector_copy(dst, src):
            nc.vector.tensor_copy(out=dst, in_=src)

        pp_t = copy_pp(turn_pp(0))
        grouped = [weights, [turn_weights(1, which, nc.scalar.copy) for which in range(2)]]
        state = turn_aa_bb(0)
        k_ps = project(wk, xk_words, xk_scales, "k")
        v_ps = project(wv, xv_words, xv_scales, "v")
        two_rhos = [two_over_bb(t) for t in range(AHEAD)]

        done = None
        for t in range(CH_TILES):
            more = t + 1 < CH_TILES
            decay = vec_cols[:, t : t + 1]
            two_rho = two_rhos[t]
            if more:
                next_state = turn_aa_bb(t + 1)
                next_pp = turn_pp(t + 1)

            d2 = late_tile("d2")
            nc.vector.scalar_tensor_tensor(
                out=d2[:], in0=k_ps[:], scalar=decay, in1=pp_t[:], op0=ALU.subtract, op1=ALU.subtract
            )
            grow_new = late_tile("grow_new")
            nc.scalar.activation(out=grow_new[:], in_=d2[:], func=ACT.Exp)
            qq2 = late_tile("qq2")
            nc.vector.scalar_tensor_tensor(
                out=qq2[:], in0=pp_t[:], scalar=decay, in1=k_ps[:], op0=ALU.add, op1=ALU.max
            )
            nc.vector.tensor_tensor(out=two_rho[:], in0=state[:, 0, :], in1=two_rho[:], op=ALU.mult)
            gate = late_tile("gate")
            nc.vector.tensor_tensor(out=gate[:], in0=d2[:], in1=log_bb[:, t, :], op=ALU.subtract)
            grow_old = late_tile("grow_old")
            nc.scalar.activation(out=grow_old[:], in_=d2[:], func=ACT.Exp, scale=-1.0)
            if more:
                wk = quantise_weights(grouped[t + 1][0], "wk")
            swing = late_tile("swing")
            nc.vector.scalar_tensor_tensor(
                out=swing[:], in0=two_rho[:], scalar=-0.5, in1=v_ps[:], op0=ALU.mult, op1=ALU.add
            )
            if more:
                next_pp_t = copy_pp(next_pp)
            if more:
                wv = quantise_weights(grouped[t + 1][1], "wv")

            if done is not None:
                bring_back(t - 1, 3, done[3], scalar_copy)
                bring_back(t - 1, 1, done[1], scalar_copy)
            nc.scalar.activation(
                out=gate[:], in_=gate[:], func=ACT.Tanh, scale=0.5, bias=half_both[:, t : t + 1]
            )
            if t + 2 < CH_TILES:
                grouped.append([turn_weights(t + 2, 0, nc.scalar.copy), turn_weights(t + 2, 1, nc.scalar.copy)])
            if more:
                k_ps = project(wk, xk_words, xk_scales, "k")
            spare = "out" if more else "turned"
            if done is not None:
                bring_back(t - 1, 2, done[2], scalar_copy, spare)
                bring_back(t - 1, 0, done[0], scalar_half, spare)
            if not more:
                bring_back(t, 3, (qq2,), scalar_copy)
            if t + AHEAD < CH_TILES:
                two_rhos.append(two_over_bb(t + AHEAD))

            e2b = late_tile("e2b")
            nc.vector.tensor_scalar(out=e2b[:], in0=grow_new[:], scalar1=1.0, scalar2=None, op0=ALU.min)
            old_aa = late_tile("old_aa")
            nc.vector.scalar_tensor_tensor(
                out=old_aa[:], in0=grow_old[:], scalar=1.0, in1=state[:, 0, :], op0=ALU.min, op1=ALU.mult
            )
            new_aa = late_tile("new_aa")
            nc.vector.tensor_tensor(out=new_aa[:], in0=e2b[:], in1=v_ps[:], op=ALU.mult)
            if not more:
                bring_back(t, 1, (old_aa, new_aa), scalar_copy)
            old_bb = late_tile("old_bb")
            nc.vector.scalar_tensor_tensor(
                out=old_bb[:], in0=grow_old[:], scalar=1.0, in1=state[:, 1, :], op0=ALU.min, op1=ALU.mult
            )
            nc.vector.scalar_tensor_tensor(
                out=swing[:], in0=gate[:], scalar=1.0, in1=swing[:], op0=ALU.add, op1=ALU.mult
            )
            if not more:
                bring_back(t, 2, (old_bb, e2b), vector_copy, spare)
            done = ((two_rho, swing), (old_aa, new_aa), (old_bb, e2b), (qq2,))
            if more:
                v_ps = project(wv, xv_words, xv_scales, "v")
                state, pp_t = next_state, next_pp_t
        bring_back(t, 0, done[0], scalar_half, spare)
